import numpy as np
import ml_dtypes


def mxq(x, axis, fmt="e4m3"):
    dtype, down = {"e4m3": (ml_dtypes.float8_e4m3fn, 7), "e5m2": (ml_dtypes.float8_e5m2, 14)}[fmt]
    v = np.moveaxis(np.asarray(x, np.float32).astype(ml_dtypes.bfloat16).astype(np.float64), axis, -1)
    blocks = v.reshape(v.shape[:-1] + (-1, 32))
    amax = np.abs(blocks).max(-1, keepdims=True)
    byte = np.maximum(np.where(amax > 0, np.frexp(amax)[1] - 1 + 127, 0) - down, 1)
    scale = np.exp2(byte - 127.0)
    codes = (blocks / scale).astype(np.float32).astype(dtype).astype(np.float64)
    return np.moveaxis((codes * scale).reshape(v.shape), -1, axis)


WIDE = False


def mx_kscale(k):
    if not WIDE:
        return np.ones(k)
    levels = np.array([10, -10, 5, -5, 0])
    a = np.random.permutation(np.resize(levels, k // 512 * 4)).reshape(k // 512, 4)
    idx = np.arange(k)
    return np.exp2(a[idx // 512, idx % 128 // 32])


BF16 = ml_dtypes.bfloat16


def bf(x):
    return np.asarray(x, np.float32).astype(BF16)


def f64(x):
    return np.asarray(x).astype(np.float64)


B, N, P, C, HID, NB, E, MAXLEN = 2, 64, 3, 256, 128, 63, 1024, 2056
F = 3 * HID + 2 * NB + 2
MIN_BIN, MAX_BIN, FAR = 0.001, 20.0, 1e8


def distogram(pos):
    d = np.sqrt(((pos[:, :, None, :] - pos[:, None, :, :]) ** 2).sum(-1))[..., None]
    lower = np.linspace(MIN_BIN, MAX_BIN, NB)
    upper = np.concatenate([lower[1:], [FAR]])
    return np.where((d > lower) & (d < upper), 1.0, 0.0)


def cross_concat(f):
    b, n, d = f.shape
    return np.concatenate([np.broadcast_to(f[:, :, None, :], (b, n, n, d)), np.broadcast_to(f[:, None, :, :], (b, n, n, d))], axis=-1)


def setup_inputs():
    s = np.array(mx_kscale(F))
    s[HID:2 * HID] = s[:HID]
    s[3 * HID:] = 1.0
    sr = s[2 * HID:3 * HID]
    th = np.random.random((B, N, N, HID // 2)) * 2.0 * np.pi
    return {"n2e": bf(np.random.standard_normal((B, N, HID)) * 0.6 * s[:HID]),
            "relpos_emb": bf(np.concatenate([np.sin(th), np.cos(th)], axis=-1)),
            "trans": bf(np.random.standard_normal((B, N, P)) * 10.0),
            "sc_trans": bf(np.random.standard_normal((B, N, P)) * 10.0),
            "flow_mask": bf(np.random.random((B, N)) > 0.5),
            "W_rp": bf(np.random.standard_normal((HID, HID)) * 0.7 / np.sqrt(HID) * sr),
            "b_rp": bf(np.random.standard_normal(HID) * 0.1 * sr),
            "W1": bf(np.random.standard_normal((F, E)) * 2.0 / np.sqrt(F) / s[:, None]),
            "b1": bf(np.random.standard_normal(E) * 0.3)}


def reference(n2e, relpos_emb, trans, sc_trans, flow_mask, W_rp, b_rp, W1, b1):
    pair_node_feats = cross_concat(f64(n2e))
    relpos_feats = f64(relpos_emb) @ f64(W_rp) + f64(b_rp)
    dist_feats = distogram(f64(trans))
    sc_feats = distogram(f64(sc_trans))
    flow_feat = cross_concat(f64(flow_mask)[..., None])
    feats = np.concatenate([pair_node_feats, relpos_feats, dist_feats, sc_feats, flow_feat], axis=-1)
    return np.maximum((mxq(feats, 3, "e4m3") @ mxq(f64(W1), 0, "e4m3")) + f64(b1), 0.0)

@@ -1,0 +1,287 @@
+from contextlib import ExitStack
+
+import concourse.mybir as mybir
+from concourse.masks import make_identity
+
+F32 = mybir.dt.float32
+BF16 = mybir.dt.bfloat16
+U32 = mybir.dt.uint32
+U8 = mybir.dt.uint8
+FP8X4 = mybir.dt.float8_e4m3fn_x4
+ALU = mybir.AluOpType
+ACT = mybir.ActivationFunctionType
+
+B, N, XYZ, HID, NB, E = 2, 64, 3, 128, 63, 1024
+F = 3 * HID + 2 * NB + 2
+MIN_BIN, MAX_BIN, FAR = 0.001, 20.0, 1e8
+
+P = 128
+PACK = 4
+QUAD = P // PACK
+BANK = 512
+JB = 4
+JS = 2
+JL = 16
+PM_RING = 3
+SLOTS = 2 * QUAD
+
+FLOPS = 2 * B * N * N * F * E + 2 * B * N * N * HID * HID
+
+
+def floor_to_float32(x):
+    mantissa, exponent = x, 0
+    while mantissa >= 2.0:
+        mantissa, exponent = mantissa / 2.0, exponent + 1
+    while mantissa < 1.0:
+        mantissa, exponent = mantissa * 2.0, exponent - 1
+    return int(mantissa * 2.0**23) / 2.0**23 * 2.0**exponent
+
+
+EDGES = [k * ((MAX_BIN - MIN_BIN) / (NB - 1)) + MIN_BIN for k in range(NB - 1)] + [MAX_BIN, FAR]
+EDGES_SQ = [edge * edge for edge in EDGES]
+STEP_AT = [floor_to_float32(sq) for sq in EDGES_SQ]
+ON_EDGE = [sq for sq in EDGES_SQ if floor_to_float32(sq) == sq]
+
+
+def tile_edgefeaturenet_pa_t_kernel(
+    tc, n2e, relpos_emb, trans, sc_trans, flow_mask, W_rp, b_rp, W1, b1, out
+):
+    nc = tc.nc
+    emb_rows = relpos_emb.rearrange("b i j c -> (b i) j c")
+    out_rows = out.rearrange("b i j e -> (b i) j e")
+
+    with ExitStack() as ctx:
+        keep = ctx.enter_context(tc.tile_pool(name="keep", bufs=1))
+        work = ctx.enter_context(tc.tile_pool(name="work", bufs=2))
+        stores = ctx.enter_context(tc.tile_pool(name="stores", bufs=4))
+        ps_emb = ctx.enter_context(tc.psum_pool(name="ps_emb", bufs=1))
+        ps_rel = ctx.enter_context(tc.psum_pool(name="ps_rel", bufs=1))
+        ps_feat = ctx.enter_context(tc.psum_pool(name="ps_feat", bufs=2))
+        ps_acc = ctx.enter_context(tc.psum_pool(name="ps_acc", bufs=4))
+
+        posi = keep.tile([P, 2, 16], BF16)
+        posj = keep.tile([P, 2, N, XYZ], BF16)
+        for g, pos in enumerate((trans, sc_trans)):
+            nc.scalar.dma_start(out=posi[:, g, 0:XYZ], in_=pos.rearrange("b i c -> (b i) c"))
+            for b in range(B):
+                nc.sync.dma_start(
+                    out=posj[b * N : (b + 1) * N, g, :, :].rearrange("p j c -> p (j c)"),
+                    in_=pos[b].rearrange("j c -> (j c)").partition_broadcast(N),
+                )
+        w1_raw = keep.tile([P, PACK, E], BF16)
+        nc.sync.dma_start(
+            out=w1_raw[0 : 3 * QUAD, :, :],
+            in_=W1[0 : 3 * HID, :].rearrange("(p t) e -> p t e", t=PACK),
+        )
+        bins = W1[3 * HID : 3 * HID + 2 * NB, :].rearrange("(g k) e -> g k e", g=2)
+        nc.scalar.dma_start(
+            out=w1_raw[3 * QUAD : P - 1, :, :].rearrange("r (g v) e -> r g v e", g=2),
+            in_=bins[:, 0 : NB - 1, :].rearrange("g (r v) e -> r g v e", v=2),
+        )
+        nc.scalar.dma_start(
+            out=w1_raw[P - 1 : P, 0:PACK:2, :], in_=bins[:, NB - 1 : NB, :].rearrange("g o e -> o g e")
+        )
+        nc.scalar.dma_start(out=w1_raw[P - 1 : P, 1:PACK:2, :], in_=W1[F - 2 : F, :].unsqueeze(0))
+        wrp_raw = keep.tile([P, HID], BF16)
+        nc.scalar.dma_start(out=wrp_raw[:], in_=W_rp)
+        brp_raw = keep.tile([P, HID], BF16)
+        nc.vector.memset(brp_raw[:], 0.0)
+        nc.scalar.dma_start(out=brp_raw[0:1, :], in_=b_rp.unsqueeze(0))
+        n2e_i = keep.tile([P, HID], BF16)
+        nc.scalar.dma_start(out=n2e_i[:], in_=n2e.rearrange("b i h -> (b i) h"))
+        flow_i = keep.tile([P, 1], BF16)
+        nc.scalar.dma_start(out=flow_i[:], in_=flow_mask.rearrange("b i -> (b i)").unsqueeze(1))
+        flow_j = keep.tile([P, N], BF16)
+        for b in range(B):
+            nc.scalar.dma_start(
+                out=flow_j[b * N : (b + 1) * N, :], in_=flow_mask[b].partition_broadcast(N)
+            )
+        b1_bf = keep.tile([P, E], BF16)
+        nc.scalar.dma_start(out=b1_bf[:], in_=b1.partition_broadcast(P))
+        emb = keep.tile([P, N, HID], BF16)
+        n2e_j = keep.tile([P, N, HID], BF16)
+        for first in range(0, N, JL):
+            js = slice(first, first + JL)
+            nc.sync.dma_start(out=emb[:, js, :], in_=emb_rows[:, js, :])
+            for b in range(B):
+                nc.sync.dma_start(
+                    out=n2e_j[b * N : (b + 1) * N, js, :].rearrange("p j h -> p (j h)"),
+                    in_=n2e[b, js, :].rearrange("j h -> (j h)").partition_broadcast(N),
+                )
+
+        step_at = keep.tile([P, SLOTS + 1], F32)
+        for k in range(SLOTS + 1):
+            nc.vector.memset(step_at[:, k : k + 1], STEP_AT[min(k, NB)])
+        ident = keep.tile([P, P], BF16)
+        make_identity(nc, ident[:])
+        ident_words = keep.tile([P, P], F32)
+        make_identity(nc, ident_words[:])
+        ones_row = keep.tile([P, P], BF16)
+        nc.vector.memset(ones_row[:], 0.0)
+        nc.vector.memset(ones_row[0:1, :], 1.0)
+
+        diff = keep.tile([P, 2, N, XYZ], F32)
+        nc.vector.tensor_tensor(
+            out=diff[:],
+            in0=posj[:],
+            in1=posi[:, :, 0:XYZ].unsqueeze(2).to_broadcast([P, 2, N, XYZ]),
+            op=ALU.subtract,
+        )
+        nc.vector.tensor_tensor(out=diff[:], in0=diff[:], in1=diff[:], op=ALU.mult)
+        dist_sq = keep.tile([P, 2, N], F32)
+        nc.vector.tensor_reduce(out=dist_sq[:], in_=diff[:], axis=mybir.AxisListType.X, op=ALU.add)
+        on_edge = keep.tile([P, 2, N], F32)
+        for sq in ON_EDGE:
+            nc.vector.tensor_scalar(
+                out=on_edge[:], in0=dist_sq[:], scalar1=sq, scalar2=-(sq + 1.0),
+                op0=ALU.is_equal, op1=ALU.mult,
+            )
+            nc.vector.tensor_tensor(out=dist_sq[:], in0=dist_sq[:], in1=on_edge[:], op=ALU.add)
+        steps = keep.tile([P, 2, N, SLOTS + 1], BF16)
+
+        def step_functions(js, count):
+            nc.vector.tensor_tensor(
+                out=steps[:, :, js, :],
+                in0=dist_sq[:, :, js].unsqueeze(3).to_broadcast([P, 2, count, SLOTS + 1]),
+                in1=step_at[:].unsqueeze(1).unsqueeze(1).to_broadcast([P, 2, count, SLOTS + 1]),
+                op=ALU.is_gt,
+            )
+
+        step_functions(slice(0, JB), JB)
+
+        wrp = keep.tile([P, HID], BF16)
+        nc.vector.tensor_copy(
+            out=wrp[:].rearrange("c (u r v) -> c u r v", u=2, v=2),
+            in_=wrp_raw[:].rearrange("c (r u v) -> c u r v", u=2, v=2),
+        )
+        brp_row = keep.tile([P, HID], BF16)
+        nc.vector.tensor_copy(
+            out=brp_row[:].rearrange("c (u r v) -> c u r v", u=2, v=2),
+            in_=brp_raw[:].rearrange("c (r u v) -> c u r v", u=2, v=2),
+        )
+
+        w1_grouped = keep.tile([P, E, PACK], BF16, align_bytes=64)
+        w1_codes = keep.tile([P, E], U32, align_bytes=64)
+        w1_scales = keep.tile([P, E], U8, align_bytes=64)
+        nc.vector.tensor_copy(
+            out=w1_grouped[:, 0:BANK, :], in_=w1_raw[:, :, 0:BANK].rearrange("p t e -> p e t")
+        )
+        nc.scalar.copy(
+            out=w1_grouped[:, BANK:E, :], in_=w1_raw[:, :, BANK:E].rearrange("p t e -> p e t")
+        )
+        step_functions(slice(JB, JL), JL - JB)
+        for e0 in range(0, E, BANK):
+            nc.vector.quantize_mx(
+                out=w1_codes[:, e0 : e0 + BANK].bitcast(FP8X4),
+                scales=w1_scales[:, e0 : e0 + BANK],
+                in_=w1_grouped[:, e0 : e0 + BANK, :].rearrange("p e t -> p (e t)"),
+            )
+        b1_rows = keep.tile([P, E], F32)
+        nc.scalar.copy(out=b1_rows[:], in_=b1_bf[:])
+        for first in range(JL, N, JL):
+            step_functions(slice(first, first + JL), JL)
+
+        pm_ring = []
+        for ring in range(PM_RING):
+            pm = keep.tile([P, JB, 2, P, 2], BF16, name="pm%d" % ring)
+            for u in range(2):
+                nc.scalar.copy(
+                    out=pm[:, :, u, 0:QUAD, :],
+                    in_=n2e_i[:].rearrange("p (r u v) -> p u r v", u=2, v=2)[:, u, :, :]
+                    .unsqueeze(1).to_broadcast([P, JB, QUAD, 2]),
+                )
+            pm_ring.append(pm)
+
+        for batch in range(N // JB):
+            j0 = batch * JB
+            pm = pm_ring[batch % PM_RING]
+            pm_words = pm[:].rearrange("p a u w v -> p (a u w v)").bitcast(F32)
+
+            emb_t_ps = ps_emb.tile([P, JB, P], BF16)
+            for a in range(JB):
+                nc.tensor.transpose(out=emb_t_ps[:, a, :], in_=emb[:, j0 + a, :], identity=ident[:])
+            emb_t = work.tile([P, JB, P], BF16)
+            nc.scalar.copy(out=emb_t[:], in_=emb_t_ps[:])
+            rel_ps = ps_rel.tile([P, JB, HID], F32)
+            for a in range(JB):
+                nc.tensor.matmul(
+                    out=rel_ps[:, a, :], lhsT=ones_row[:], rhs=brp_row[:], start=True, stop=False
+                )
+                nc.tensor.matmul(
+                    out=rel_ps[:, a, :], lhsT=emb_t[:, a, :], rhs=wrp[:], start=False, stop=True
+                )
+            nc.scalar.copy(
+                out=pm[:, :, :, 2 * QUAD : 3 * QUAD, :].rearrange("p a u r v -> p a u (r v)"),
+                in_=rel_ps[:].rearrange("p a (u x) -> p a u x", u=2),
+            )
+            for u in range(2):
+                nc.gpsimd.tensor_scalar(
+                    out=pm[:, :, u, QUAD : 2 * QUAD, :],
+                    in0=n2e_j[:, j0 : j0 + JB, :].rearrange(
+                        "p a (r u v) -> p a u r v", u=2, v=2
+                    )[:, :, u, :, :],
+                    scalar1=1.0, scalar2=0.0, op0=ALU.mult, op1=ALU.add,
+                )
+            nc.gpsimd.tensor_tensor(
+                out=pm[:, :, :, 3 * QUAD : P, :].rearrange("p a g r v -> p a g (r v)"),
+                in0=steps[:, :, j0 : j0 + JB, 0:SLOTS].rearrange("p g a s -> p a g s"),
+                in1=steps[:, :, j0 : j0 + JB, 1 : SLOTS + 1].rearrange("p g a s -> p a g s"),
+                op=ALU.subtract,
+            )
+            nc.gpsimd.tensor_copy(
+                out=pm[:, :, 0, P - 1, 1:2], in_=flow_i[:].unsqueeze(1).to_broadcast([P, JB, 1])
+            )
+            nc.gpsimd.tensor_copy(
+                out=pm[:, :, 1, P - 1, 1:2], in_=flow_j[:, j0 : j0 + JB].unsqueeze(2)
+            )
+
+            grouped = work.tile([P, JB, P, PACK], BF16, align_bytes=64)
+            grouped_words = grouped[:].rearrange("p a n t -> p (a n t)").bitcast(F32)
+            for a0 in range(0, JB, 2):
+                feat_ps = ps_feat.tile([P, 2, 2, P], F32)
+                for a in range(2):
+                    for u in range(2):
+                        w0 = ((a0 + a) * 2 + u) * P
+                        nc.tensor.transpose(
+                            out=feat_ps[:, a, u, :], in_=pm_words[:, w0 : w0 + P],
+                            identity=ident_words[:],
+                        )
+                nc.scalar.copy(
+                    out=grouped_words[:, a0 * 2 * P : (a0 + 2) * 2 * P].rearrange(
+                        "p (a n u) -> p a n u", a=2, u=2
+                    ),
+                    in_=feat_ps[:].rearrange("p a u n -> p a n u"),
+                )
+            codes = work.tile([P, JB * P], U32, align_bytes=64)
+            scales = work.tile([P, JB * P], U8, align_bytes=64)
+            nc.vector.quantize_mx(
+                out=codes[:].bitcast(FP8X4),
+                scales=scales[:],
+                in_=grouped[:].rearrange("p a n t -> p (a n t)"),
+            )
+
+            for a0 in range(0, JB, JS):
+                result = stores.tile([P, JS, E], F32)
+                for a in range(JS):
+                    pairs = slice((a0 + a) * P, (a0 + a + 1) * P)
+                    for e0 in range(0, E, BANK):
+                        acc = ps_acc.tile([P, BANK], F32)
+                        nc.tensor.matmul_mx(
+                            out=acc[:],
+                            lhsT=codes[:, pairs].bitcast(FP8X4),
+                            lhsT_scale=scales[:, pairs],
+                            rhs=w1_codes[:, e0 : e0 + BANK].bitcast(FP8X4),
+                            rhs_scale=w1_scales[:, e0 : e0 + BANK],
+                            start=True,
+                            stop=True,
+                        )
+                        nc.vector.tensor_tensor(
+                            out=result[:, a, e0 : e0 + BANK], in0=acc[:],
+                            in1=b1_rows[:, e0 : e0 + BANK], op=ALU.add,
+                        )
+                nc.scalar.activation(out=result[:, 0, :], in_=result[:, 0, :], func=ACT.Relu)
+                nc.gpsimd.tensor_scalar(
+                    out=result[:, 1, :], in0=result[:, 1, :],
+                    scalar1=0.0, scalar2=0.0, op0=ALU.max, op1=ALU.add,
+                )
+                nc.sync.dma_start(out=out_rows[:, j0 + a0 : j0 + a0 + JS, :], in_=result[:])

@@ -282,6 +282,6 @@ def tile_edgefeaturenet_pa_t_kernel(
                 nc.scalar.activation(out=result[:, 0, :], in_=result[:, 0, :], func=ACT.Relu)
                 nc.gpsimd.tensor_scalar(
                     out=result[:, 1, :], in0=result[:, 1, :],
-                    scalar1=0.0, scalar2=0.0, op0=ALU.max, op1=ALU.add,
+                    scalar1=float("inf"), scalar2=0.0, op0=ALU.min, op1=ALU.max,
                 )
                 nc.sync.dma_start(out=out_rows[:, j0 + a0 : j0 + a0 + JS, :], in_=result[:])

@@ -17,13 +17,12 @@ MIN_BIN, MAX_BIN, FAR = 0.001, 20.0, 1e8
 
 P = 128
 PACK = 4
-QUAD = P // PACK
 BANK = 512
 JB = 4
 JS = 2
-JL = 16
+JL = (N - JB) // 3
 PM_RING = 3
-SLOTS = 2 * QUAD
+BATCHES = N // JB
 
 FLOPS = 2 * B * N * N * F * E + 2 * B * N * N * HID * HID
 
@@ -51,6 +50,7 @@ def tile_edgefeaturenet_pa_t_kernel(
     out_rows = out.rearrange("b i j e -> (b i) j e")
 
     with ExitStack() as ctx:
+        ctx.enter_context(tc.manual_schedule())
         keep = ctx.enter_context(tc.tile_pool(name="keep", bufs=1))
         work = ctx.enter_context(tc.tile_pool(name="work", bufs=2))
         stores = ctx.enter_context(tc.tile_pool(name="stores", bufs=4))
@@ -68,27 +68,27 @@ def tile_edgefeaturenet_pa_t_kernel(
                     out=posj[b * N : (b + 1) * N, g, :, :].rearrange("p j c -> p (j c)"),
                     in_=pos[b].rearrange("j c -> (j c)").partition_broadcast(N),
                 )
-        w1_raw = keep.tile([P, PACK, E], BF16)
-        nc.sync.dma_start(
-            out=w1_raw[0 : 3 * QUAD, :, :],
-            in_=W1[0 : 3 * HID, :].rearrange("(p t) e -> p t e", t=PACK),
-        )
-        bins = W1[3 * HID : 3 * HID + 2 * NB, :].rearrange("(g k) e -> g k e", g=2)
-        nc.scalar.dma_start(
-            out=w1_raw[3 * QUAD : P - 1, :, :].rearrange("r (g v) e -> r g v e", g=2),
-            in_=bins[:, 0 : NB - 1, :].rearrange("g (r v) e -> r g v e", v=2),
-        )
-        nc.scalar.dma_start(
-            out=w1_raw[P - 1 : P, 0:PACK:2, :], in_=bins[:, NB - 1 : NB, :].rearrange("g o e -> o g e")
-        )
-        nc.scalar.dma_start(out=w1_raw[P - 1 : P, 1:PACK:2, :], in_=W1[F - 2 : F, :].unsqueeze(0))
-        wrp_raw = keep.tile([P, HID], BF16)
-        nc.scalar.dma_start(out=wrp_raw[:], in_=W_rp)
-        brp_raw = keep.tile([P, HID], BF16)
-        nc.vector.memset(brp_raw[:], 0.0)
-        nc.scalar.dma_start(out=brp_raw[0:1, :], in_=b_rp.unsqueeze(0))
+        wrp = keep.tile([P, HID], BF16)
+        nc.scalar.dma_start(out=wrp[:], in_=W_rp)
+        brp_row = keep.tile([P, HID], BF16)
+        nc.vector.memset(brp_row[:], 0.0)
+        nc.scalar.dma_start(out=brp_row[0:1, :], in_=b_rp.unsqueeze(0))
         n2e_i = keep.tile([P, HID], BF16)
         nc.scalar.dma_start(out=n2e_i[:], in_=n2e.rearrange("b i h -> (b i) h"))
+        emb = keep.tile([P, N, HID], BF16)
+        n2e_j = keep.tile([P, N, HID], BF16)
+
+        def load_pairs(js):
+            nc.sync.dma_start(out=emb[:, js, :], in_=emb_rows[:, js, :])
+            for b in range(B):
+                nc.sync.dma_start(
+                    out=n2e_j[b * N : (b + 1) * N, js, :].rearrange("p j h -> p (j h)"),
+                    in_=n2e[b, js, :].rearrange("j h -> (j h)").partition_broadcast(N),
+                )
+
+        load_pairs(slice(0, JB))
+        w1_raw = keep.tile([P, PACK, E], BF16)
+        nc.sync.dma_start(out=w1_raw[:], in_=W1.rearrange("(p t) e -> p t e", t=PACK))
         flow_i = keep.tile([P, 1], BF16)
         nc.scalar.dma_start(out=flow_i[:], in_=flow_mask.rearrange("b i -> (b i)").unsqueeze(1))
         flow_j = keep.tile([P, N], BF16)
@@ -98,20 +98,12 @@ def tile_edgefeaturenet_pa_t_kernel(
             )
         b1_bf = keep.tile([P, E], BF16)
         nc.scalar.dma_start(out=b1_bf[:], in_=b1.partition_broadcast(P))
-        emb = keep.tile([P, N, HID], BF16)
-        n2e_j = keep.tile([P, N, HID], BF16)
-        for first in range(0, N, JL):
-            js = slice(first, first + JL)
-            nc.sync.dma_start(out=emb[:, js, :], in_=emb_rows[:, js, :])
-            for b in range(B):
-                nc.sync.dma_start(
-                    out=n2e_j[b * N : (b + 1) * N, js, :].rearrange("p j h -> p (j h)"),
-                    in_=n2e[b, js, :].rearrange("j h -> (j h)").partition_broadcast(N),
-                )
+        for first in range(JB, N, JL):
+            load_pairs(slice(first, first + JL))
 
-        step_at = keep.tile([P, SLOTS + 1], F32)
-        for k in range(SLOTS + 1):
-            nc.vector.memset(step_at[:, k : k + 1], STEP_AT[min(k, NB)])
+        step_at = keep.tile([P, NB + 1], F32)
+        for k in range(NB + 1):
+            nc.vector.memset(step_at[:, k : k + 1], STEP_AT[k])
         ident = keep.tile([P, P], BF16)
         make_identity(nc, ident[:])
         ident_words = keep.tile([P, P], F32)
@@ -119,6 +111,17 @@ def tile_edgefeaturenet_pa_t_kernel(
         ones_row = keep.tile([P, P], BF16)
         nc.vector.memset(ones_row[:], 0.0)
         nc.vector.memset(ones_row[0:1, :], 1.0)
+
+        pm_ring = []
+        for ring in range(PM_RING):
+            pm = keep.tile([P, JB, F], BF16, name="pm%d" % ring)
+            nc.scalar.copy(
+                out=pm[:, :, 0:HID], in_=n2e_i[:].unsqueeze(1).to_broadcast([P, JB, HID])
+            )
+            nc.gpsimd.tensor_copy(
+                out=pm[:, :, F - 2 : F - 1], in_=flow_i[:].unsqueeze(1).to_broadcast([P, JB, 1])
+            )
+            pm_ring.append(pm)
 
         diff = keep.tile([P, 2, N, XYZ], F32)
         nc.vector.tensor_tensor(
@@ -137,29 +140,117 @@ def tile_edgefeaturenet_pa_t_kernel(
                 op0=ALU.is_equal, op1=ALU.mult,
             )
             nc.vector.tensor_tensor(out=dist_sq[:], in0=dist_sq[:], in1=on_edge[:], op=ALU.add)
-        steps = keep.tile([P, 2, N, SLOTS + 1], BF16)
 
-        def step_functions(js, count):
+        emb_t_of = {}
+        grouped_of = {}
+        codes_of = {}
+
+        def transpose_emb(batch):
+            emb_t_ps = ps_emb.tile([P, JB, P], BF16)
+            for a in range(JB):
+                nc.tensor.transpose(
+                    out=emb_t_ps[:, a, :], in_=emb[:, batch * JB + a, :], identity=ident[:]
+                )
+            emb_t = work.tile([P, JB, P], BF16)
+            nc.scalar.copy(out=emb_t[:], in_=emb_t_ps[:])
+            emb_t_of[batch] = emb_t
+
+        def pair_features(batch):
+            js = slice(batch * JB, (batch + 1) * JB)
+            pm = pm_ring[batch % PM_RING]
+            emb_t = emb_t_of[batch]
+            rel_ps = ps_rel.tile([P, JB, HID], F32)
+            for a in range(JB):
+                nc.tensor.matmul(
+                    out=rel_ps[:, a, :], lhsT=ones_row[:], rhs=brp_row[:], start=True, stop=False
+                )
+                nc.tensor.matmul(
+                    out=rel_ps[:, a, :], lhsT=emb_t[:, a, :], rhs=wrp[:], start=False, stop=True
+                )
+            nc.scalar.copy(out=pm[:, :, 2 * HID : 3 * HID], in_=rel_ps[:])
+            nc.gpsimd.tensor_scalar(
+                out=pm[:, :, HID : 2 * HID], in0=n2e_j[:, js, :],
+                scalar1=1.0, scalar2=0.0, op0=ALU.mult, op1=ALU.add,
+            )
+            steps = work.tile([P, 2, JB, NB + 1], BF16)
             nc.vector.tensor_tensor(
-                out=steps[:, :, js, :],
-                in0=dist_sq[:, :, js].unsqueeze(3).to_broadcast([P, 2, count, SLOTS + 1]),
-                in1=step_at[:].unsqueeze(1).unsqueeze(1).to_broadcast([P, 2, count, SLOTS + 1]),
+                out=steps[:],
+                in0=dist_sq[:, :, js].unsqueeze(3).to_broadcast([P, 2, JB, NB + 1]),
+                in1=step_at[:].unsqueeze(1).unsqueeze(1).to_broadcast([P, 2, JB, NB + 1]),
                 op=ALU.is_gt,
             )
+            nc.gpsimd.tensor_tensor(
+                out=pm[:, :, 3 * HID : 3 * HID + 2 * NB].rearrange("p a (g k) -> p a g k", g=2),
+                in0=steps[:, :, :, 0:NB].rearrange("p g a k -> p a g k"),
+                in1=steps[:, :, :, 1 : NB + 1].rearrange("p g a k -> p a g k"),
+                op=ALU.subtract,
+            )
+            nc.gpsimd.tensor_copy(out=pm[:, :, F - 1 : F], in_=flow_j[:, js].unsqueeze(2))
 
-        step_functions(slice(0, JB), JB)
+        def features_to_partitions(batch):
+            pm_words = pm_ring[batch % PM_RING][:].rearrange("p a k -> p (a k)").bitcast(F32)
+            grouped = work.tile([P, JB, P, PACK], BF16, align_bytes=64)
+            grouped_words = grouped[:].rearrange("p a n t -> p (a n t)").bitcast(F32)
+            for a0 in range(0, JB, 2):
+                feat_ps = ps_feat.tile([P, 2, 2, P], F32)
+                for a in range(2):
+                    for u in range(2):
+                        w0 = (a0 + a) * 2 * P
+                        nc.tensor.transpose(
+                            out=feat_ps[:, a, u, :], in_=pm_words[:, w0 + u : w0 + 2 * P : 2],
+                            identity=ident_words[:],
+                        )
+                nc.scalar.copy(
+                    out=grouped_words[:, a0 * 2 * P : (a0 + 2) * 2 * P].rearrange(
+                        "p (a n u) -> p a n u", a=2, u=2
+                    ),
+                    in_=feat_ps[:].rearrange("p a u n -> p a n u"),
+                )
+            grouped_of[batch] = grouped
 
-        wrp = keep.tile([P, HID], BF16)
-        nc.vector.tensor_copy(
-            out=wrp[:].rearrange("c (u r v) -> c u r v", u=2, v=2),
-            in_=wrp_raw[:].rearrange("c (r u v) -> c u r v", u=2, v=2),
-        )
-        brp_row = keep.tile([P, HID], BF16)
-        nc.vector.tensor_copy(
-            out=brp_row[:].rearrange("c (u r v) -> c u r v", u=2, v=2),
-            in_=brp_raw[:].rearrange("c (r u v) -> c u r v", u=2, v=2),
-        )
+        def quantise(batch):
+            grouped = grouped_of[batch]
+            codes = work.tile([P, JB * P], U32, align_bytes=64)
+            scales = work.tile([P, JB * P], U8, align_bytes=64)
+            nc.vector.quantize_mx(
+                out=codes[:].bitcast(FP8X4),
+                scales=scales[:],
+                in_=grouped[:].rearrange("p a n t -> p (a n t)"),
+            )
+            codes_of[batch] = (codes, scales)
 
+        def multiply(batch, a0):
+            codes, scales = codes_of[batch]
+            result = stores.tile([P, JS, E], F32)
+            for a in range(JS):
+                pairs = slice((a0 + a) * P, (a0 + a + 1) * P)
+                for e0 in range(0, E, BANK):
+                    acc = ps_acc.tile([P, BANK], F32)
+                    nc.tensor.matmul_mx(
+                        out=acc[:],
+                        lhsT=codes[:, pairs].bitcast(FP8X4),
+                        lhsT_scale=scales[:, pairs],
+                        rhs=w1_codes[:, e0 : e0 + BANK].bitcast(FP8X4),
+                        rhs_scale=w1_scales[:, e0 : e0 + BANK],
+                        start=True,
+                        stop=True,
+                    )
+                    nc.vector.tensor_tensor(
+                        out=result[:, a, e0 : e0 + BANK], in0=acc[:],
+                        in1=b1_rows[:, e0 : e0 + BANK], op=ALU.add,
+                    )
+            nc.scalar.activation(out=result[:, 0, :], in_=result[:, 0, :], func=ACT.Relu)
+            nc.gpsimd.tensor_scalar(
+                out=result[:, 1, :], in0=result[:, 1, :],
+                scalar1=float("inf"), scalar2=0.0, op0=ALU.min, op1=ALU.max,
+            )
+            j0 = batch * JB + a0
+            nc.sync.dma_start(out=out_rows[:, j0 : j0 + JS, :], in_=result[:])
+
+        transpose_emb(0)
+        pair_features(0)
+        transpose_emb(1)
+        features_to_partitions(0)
         w1_grouped = keep.tile([P, E, PACK], BF16, align_bytes=64)
         w1_codes = keep.tile([P, E], U32, align_bytes=64)
         w1_scales = keep.tile([P, E], U8, align_bytes=64)
@@ -169,119 +260,29 @@ def tile_edgefeaturenet_pa_t_kernel(
         nc.scalar.copy(
             out=w1_grouped[:, BANK:E, :], in_=w1_raw[:, :, BANK:E].rearrange("p t e -> p e t")
         )
-        step_functions(slice(JB, JL), JL - JB)
+        b1_rows = keep.tile([P, E], F32)
+        nc.scalar.copy(out=b1_rows[:], in_=b1_bf[:])
+        quantise(0)
         for e0 in range(0, E, BANK):
             nc.vector.quantize_mx(
                 out=w1_codes[:, e0 : e0 + BANK].bitcast(FP8X4),
                 scales=w1_scales[:, e0 : e0 + BANK],
                 in_=w1_grouped[:, e0 : e0 + BANK, :].rearrange("p e t -> p (e t)"),
             )
-        b1_rows = keep.tile([P, E], F32)
-        nc.scalar.copy(out=b1_rows[:], in_=b1_bf[:])
-        for first in range(JL, N, JL):
-            step_functions(slice(first, first + JL), JL)
+        pair_features(1)
+        transpose_emb(2)
+        features_to_partitions(1)
+        pair_features(2)
+        transpose_emb(3)
 
-        pm_ring = []
-        for ring in range(PM_RING):
-            pm = keep.tile([P, JB, 2, P, 2], BF16, name="pm%d" % ring)
-            for u in range(2):
-                nc.scalar.copy(
-                    out=pm[:, :, u, 0:QUAD, :],
-                    in_=n2e_i[:].rearrange("p (r u v) -> p u r v", u=2, v=2)[:, u, :, :]
-                    .unsqueeze(1).to_broadcast([P, JB, QUAD, 2]),
-                )
-            pm_ring.append(pm)
-
-        for batch in range(N // JB):
-            j0 = batch * JB
-            pm = pm_ring[batch % PM_RING]
-            pm_words = pm[:].rearrange("p a u w v -> p (a u w v)").bitcast(F32)
-
-            emb_t_ps = ps_emb.tile([P, JB, P], BF16)
-            for a in range(JB):
-                nc.tensor.transpose(out=emb_t_ps[:, a, :], in_=emb[:, j0 + a, :], identity=ident[:])
-            emb_t = work.tile([P, JB, P], BF16)
-            nc.scalar.copy(out=emb_t[:], in_=emb_t_ps[:])
-            rel_ps = ps_rel.tile([P, JB, HID], F32)
-            for a in range(JB):
-                nc.tensor.matmul(
-                    out=rel_ps[:, a, :], lhsT=ones_row[:], rhs=brp_row[:], start=True, stop=False
-                )
-                nc.tensor.matmul(
-                    out=rel_ps[:, a, :], lhsT=emb_t[:, a, :], rhs=wrp[:], start=False, stop=True
-                )
-            nc.scalar.copy(
-                out=pm[:, :, :, 2 * QUAD : 3 * QUAD, :].rearrange("p a u r v -> p a u (r v)"),
-                in_=rel_ps[:].rearrange("p a (u x) -> p a u x", u=2),
-            )
-            for u in range(2):
-                nc.gpsimd.tensor_scalar(
-                    out=pm[:, :, u, QUAD : 2 * QUAD, :],
-                    in0=n2e_j[:, j0 : j0 + JB, :].rearrange(
-                        "p a (r u v) -> p a u r v", u=2, v=2
-                    )[:, :, u, :, :],
-                    scalar1=1.0, scalar2=0.0, op0=ALU.mult, op1=ALU.add,
-                )
-            nc.gpsimd.tensor_tensor(
-                out=pm[:, :, :, 3 * QUAD : P, :].rearrange("p a g r v -> p a g (r v)"),
-                in0=steps[:, :, j0 : j0 + JB, 0:SLOTS].rearrange("p g a s -> p a g s"),
-                in1=steps[:, :, j0 : j0 + JB, 1 : SLOTS + 1].rearrange("p g a s -> p a g s"),
-                op=ALU.subtract,
-            )
-            nc.gpsimd.tensor_copy(
-                out=pm[:, :, 0, P - 1, 1:2], in_=flow_i[:].unsqueeze(1).to_broadcast([P, JB, 1])
-            )
-            nc.gpsimd.tensor_copy(
-                out=pm[:, :, 1, P - 1, 1:2], in_=flow_j[:, j0 : j0 + JB].unsqueeze(2)
-            )
-
-            grouped = work.tile([P, JB, P, PACK], BF16, align_bytes=64)
-            grouped_words = grouped[:].rearrange("p a n t -> p (a n t)").bitcast(F32)
-            for a0 in range(0, JB, 2):
-                feat_ps = ps_feat.tile([P, 2, 2, P], F32)
-                for a in range(2):
-                    for u in range(2):
-                        w0 = ((a0 + a) * 2 + u) * P
-                        nc.tensor.transpose(
-                            out=feat_ps[:, a, u, :], in_=pm_words[:, w0 : w0 + P],
-                            identity=ident_words[:],
-                        )
-                nc.scalar.copy(
-                    out=grouped_words[:, a0 * 2 * P : (a0 + 2) * 2 * P].rearrange(
-                        "p (a n u) -> p a n u", a=2, u=2
-                    ),
-                    in_=feat_ps[:].rearrange("p a u n -> p a n u"),
-                )
-            codes = work.tile([P, JB * P], U32, align_bytes=64)
-            scales = work.tile([P, JB * P], U8, align_bytes=64)
-            nc.vector.quantize_mx(
-                out=codes[:].bitcast(FP8X4),
-                scales=scales[:],
-                in_=grouped[:].rearrange("p a n t -> p (a n t)"),
-            )
-
-            for a0 in range(0, JB, JS):
-                result = stores.tile([P, JS, E], F32)
-                for a in range(JS):
-                    pairs = slice((a0 + a) * P, (a0 + a + 1) * P)
-                    for e0 in range(0, E, BANK):
-                        acc = ps_acc.tile([P, BANK], F32)
-                        nc.tensor.matmul_mx(
-                            out=acc[:],
-                            lhsT=codes[:, pairs].bitcast(FP8X4),
-                            lhsT_scale=scales[:, pairs],
-                            rhs=w1_codes[:, e0 : e0 + BANK].bitcast(FP8X4),
-                            rhs_scale=w1_scales[:, e0 : e0 + BANK],
-                            start=True,
-                            stop=True,
-                        )
-                        nc.vector.tensor_tensor(
-                            out=result[:, a, e0 : e0 + BANK], in0=acc[:],
-                            in1=b1_rows[:, e0 : e0 + BANK], op=ALU.add,
-                        )
-                nc.scalar.activation(out=result[:, 0, :], in_=result[:, 0, :], func=ACT.Relu)
-                nc.gpsimd.tensor_scalar(
-                    out=result[:, 1, :], in0=result[:, 1, :],
-                    scalar1=float("inf"), scalar2=0.0, op0=ALU.min, op1=ALU.max,
-                )
-                nc.sync.dma_start(out=out_rows[:, j0 + a0 : j0 + a0 + JS, :], in_=result[:])
+        for batch in range(BATCHES):
+            multiply(batch, 0)
+            if batch + 2 < BATCHES:
+                features_to_partitions(batch + 2)
+            if batch + 1 < BATCHES:
+                quantise(batch + 1)
+            multiply(batch, JS)
+            if batch + 3 < BATCHES:
+                pair_features(batch + 3)
+            if batch + 4 < BATCHES:
+                transpose_emb(batch + 4)

@@ -168,10 +168,7 @@ def tile_edgefeaturenet_pa_t_kernel(
                     out=rel_ps[:, a, :], lhsT=emb_t[:, a, :], rhs=wrp[:], start=False, stop=True
                 )
             nc.scalar.copy(out=pm[:, :, 2 * HID : 3 * HID], in_=rel_ps[:])
-            nc.gpsimd.tensor_scalar(
-                out=pm[:, :, HID : 2 * HID], in0=n2e_j[:, js, :],
-                scalar1=1.0, scalar2=0.0, op0=ALU.mult, op1=ALU.add,
-            )
+            nc.scalar.copy(out=pm[:, :, HID : 2 * HID], in_=n2e_j[:, js, :])
             steps = work.tile([P, 2, JB, NB + 1], BF16)
             nc.vector.tensor_tensor(
                 out=steps[:],
@@ -250,7 +247,6 @@ def tile_edgefeaturenet_pa_t_kernel(
         transpose_emb(0)
         pair_features(0)
         transpose_emb(1)
-        features_to_partitions(0)
         w1_grouped = keep.tile([P, E, PACK], BF16, align_bytes=64)
         w1_codes = keep.tile([P, E], U32, align_bytes=64)
         w1_scales = keep.tile([P, E], U8, align_bytes=64)
@@ -260,29 +256,30 @@ def tile_edgefeaturenet_pa_t_kernel(
         nc.scalar.copy(
             out=w1_grouped[:, BANK:E, :], in_=w1_raw[:, :, BANK:E].rearrange("p t e -> p e t")
         )
-        b1_rows = keep.tile([P, E], F32)
-        nc.scalar.copy(out=b1_rows[:], in_=b1_bf[:])
-        quantise(0)
+        pair_features(1)
+        transpose_emb(2)
+        features_to_partitions(0)
         for e0 in range(0, E, BANK):
             nc.vector.quantize_mx(
                 out=w1_codes[:, e0 : e0 + BANK].bitcast(FP8X4),
                 scales=w1_scales[:, e0 : e0 + BANK],
                 in_=w1_grouped[:, e0 : e0 + BANK, :].rearrange("p e t -> p (e t)"),
             )
-        pair_features(1)
-        transpose_emb(2)
-        features_to_partitions(1)
+        b1_rows = keep.tile([P, E], F32)
+        nc.scalar.copy(out=b1_rows[:], in_=b1_bf[:])
         pair_features(2)
         transpose_emb(3)
+        quantise(0)
+        features_to_partitions(1)
 
         for batch in range(BATCHES):
             multiply(batch, 0)
-            if batch + 2 < BATCHES:
-                features_to_partitions(batch + 2)
-            if batch + 1 < BATCHES:
-                quantise(batch + 1)
-            multiply(batch, JS)
             if batch + 3 < BATCHES:
                 pair_features(batch + 3)
             if batch + 4 < BATCHES:
                 transpose_emb(batch + 4)
+            if batch + 1 < BATCHES:
+                quantise(batch + 1)
+            multiply(batch, JS)
+            if batch + 2 < BATCHES:
+                features_to_partitions(batch + 2)

@@ -22,6 +22,7 @@ JB = 4
 JS = 2
 JL = (N - JB) // 3
 PM_RING = 3
+EDGES_ON_VECTOR = 40
 BATCHES = N // JB
 
 FLOPS = 2 * B * N * N * F * E + 2 * B * N * N * HID * HID
@@ -59,51 +60,51 @@ def tile_edgefeaturenet_pa_t_kernel(
         ps_feat = ctx.enter_context(tc.psum_pool(name="ps_feat", bufs=2))
         ps_acc = ctx.enter_context(tc.psum_pool(name="ps_acc", bufs=4))
 
-        posi = keep.tile([P, 2, 16], BF16)
-        posj = keep.tile([P, 2, N, XYZ], BF16)
-        for g, pos in enumerate((trans, sc_trans)):
-            nc.scalar.dma_start(out=posi[:, g, 0:XYZ], in_=pos.rearrange("b i c -> (b i) c"))
-            for b in range(B):
-                nc.sync.dma_start(
-                    out=posj[b * N : (b + 1) * N, g, :, :].rearrange("p j c -> p (j c)"),
-                    in_=pos[b].rearrange("j c -> (j c)").partition_broadcast(N),
-                )
-        wrp = keep.tile([P, HID], BF16)
-        nc.scalar.dma_start(out=wrp[:], in_=W_rp)
-        brp_row = keep.tile([P, HID], BF16)
-        nc.vector.memset(brp_row[:], 0.0)
-        nc.scalar.dma_start(out=brp_row[0:1, :], in_=b_rp.unsqueeze(0))
-        n2e_i = keep.tile([P, HID], BF16)
-        nc.scalar.dma_start(out=n2e_i[:], in_=n2e.rearrange("b i h -> (b i) h"))
         emb = keep.tile([P, N, HID], BF16)
         n2e_j = keep.tile([P, N, HID], BF16)
 
-        def load_pairs(js):
+        def load_emb(js):
             nc.sync.dma_start(out=emb[:, js, :], in_=emb_rows[:, js, :])
+
+        def load_nodes(js):
             for b in range(B):
                 nc.sync.dma_start(
                     out=n2e_j[b * N : (b + 1) * N, js, :].rearrange("p j h -> p (j h)"),
                     in_=n2e[b, js, :].rearrange("j h -> (j h)").partition_broadcast(N),
                 )
 
-        load_pairs(slice(0, JB))
+        load_emb(slice(0, JB))
+        pos_all = keep.tile([P, 2, B, N, XYZ], BF16)
+        posi = keep.tile([P, 2, 16], BF16)
+        for g, pos in enumerate((trans, sc_trans)):
+            nc.sync.dma_start(
+                out=pos_all[:, g, :, :, :].rearrange("p b j c -> p (b j c)"),
+                in_=pos.rearrange("b j c -> (b j c)").partition_broadcast(P),
+            )
+            nc.sync.dma_start(out=posi[:, g, 0:XYZ], in_=pos.rearrange("b i c -> (b i) c"))
+        wrp = keep.tile([P, HID], BF16)
+        nc.sync.dma_start(out=wrp[:], in_=W_rp)
+        brp_row = keep.tile([P, HID], BF16)
+        nc.vector.memset(brp_row[:], 0.0)
+        nc.sync.dma_start(out=brp_row[0:1, :], in_=b_rp.unsqueeze(0))
         w1_raw = keep.tile([P, PACK, E], BF16)
         nc.sync.dma_start(out=w1_raw[:], in_=W1.rearrange("(p t) e -> p t e", t=PACK))
+        n2e_i = keep.tile([P, HID], BF16)
+        nc.sync.dma_start(out=n2e_i[:], in_=n2e.rearrange("b i h -> (b i) h"))
+        load_nodes(slice(0, JB))
         flow_i = keep.tile([P, 1], BF16)
-        nc.scalar.dma_start(out=flow_i[:], in_=flow_mask.rearrange("b i -> (b i)").unsqueeze(1))
-        flow_j = keep.tile([P, N], BF16)
-        for b in range(B):
-            nc.scalar.dma_start(
-                out=flow_j[b * N : (b + 1) * N, :], in_=flow_mask[b].partition_broadcast(N)
-            )
+        nc.sync.dma_start(out=flow_i[:], in_=flow_mask.rearrange("b i -> (b i)").unsqueeze(1))
+        flow_all = keep.tile([P, B, N], BF16)
+        nc.sync.dma_start(
+            out=flow_all[:].rearrange("p b j -> p (b j)"),
+            in_=flow_mask.rearrange("b j -> (b j)").partition_broadcast(P),
+        )
         b1_bf = keep.tile([P, E], BF16)
-        nc.scalar.dma_start(out=b1_bf[:], in_=b1.partition_broadcast(P))
+        nc.sync.dma_start(out=b1_bf[:], in_=b1.partition_broadcast(P))
         for first in range(JB, N, JL):
-            load_pairs(slice(first, first + JL))
+            load_emb(slice(first, first + JL))
+            load_nodes(slice(first, first + JL))
 
-        step_at = keep.tile([P, NB + 1], F32)
-        for k in range(NB + 1):
-            nc.vector.memset(step_at[:, k : k + 1], STEP_AT[k])
         ident = keep.tile([P, P], BF16)
         make_identity(nc, ident[:])
         ident_words = keep.tile([P, P], F32)
@@ -111,25 +112,47 @@ def tile_edgefeaturenet_pa_t_kernel(
         ones_row = keep.tile([P, P], BF16)
         nc.vector.memset(ones_row[:], 0.0)
         nc.vector.memset(ones_row[0:1, :], 1.0)
+        flow_j = keep.tile([P, N], BF16)
+        for b in range(B):
+            nc.gpsimd.tensor_copy(
+                out=flow_j[b * N : (b + 1) * N, :], in_=flow_all[b * N : (b + 1) * N, b, :]
+            )
+        step_at = keep.tile([P, NB + 1], F32)
+        zero = keep.tile([P, 1], F32)
+        nc.vector.memset(zero[:], 0.0)
+        for k in range(NB + 1):
+            if k < EDGES_ON_VECTOR:
+                nc.vector.memset(step_at[:, k : k + 1], STEP_AT[k])
+            else:
+                nc.scalar.activation(
+                    out=step_at[:, k : k + 1], in_=zero[:], func=ACT.Copy, bias=STEP_AT[k], scale=1.0
+                )
 
         pm_ring = []
         for ring in range(PM_RING):
             pm = keep.tile([P, JB, F], BF16, name="pm%d" % ring)
-            nc.scalar.copy(
-                out=pm[:, :, 0:HID], in_=n2e_i[:].unsqueeze(1).to_broadcast([P, JB, HID])
-            )
-            nc.gpsimd.tensor_copy(
-                out=pm[:, :, F - 2 : F - 1], in_=flow_i[:].unsqueeze(1).to_broadcast([P, JB, 1])
-            )
             pm_ring.append(pm)
 
+        def constant_node_features(ring):
+            nc.scalar.copy(
+                out=pm_ring[ring][:, :, 0:HID], in_=n2e_i[:].unsqueeze(1).to_broadcast([P, JB, HID])
+            )
+
+        def constant_flag(ring, small):
+            small.tensor_copy(
+                out=pm_ring[ring][:, :, F - 2 : F - 1],
+                in_=flow_i[:].unsqueeze(1).to_broadcast([P, JB, 1]),
+            )
+
         diff = keep.tile([P, 2, N, XYZ], F32)
-        nc.vector.tensor_tensor(
-            out=diff[:],
-            in0=posj[:],
-            in1=posi[:, :, 0:XYZ].unsqueeze(2).to_broadcast([P, 2, N, XYZ]),
-            op=ALU.subtract,
-        )
+        for b in range(B):
+            rows = slice(b * N, (b + 1) * N)
+            nc.vector.tensor_tensor(
+                out=diff[rows, :, :, :],
+                in0=pos_all[rows, :, b, :, :],
+                in1=posi[rows, :, 0:XYZ].unsqueeze(2).to_broadcast([N, 2, N, XYZ]),
+                op=ALU.subtract,
+            )
         nc.vector.tensor_tensor(out=diff[:], in0=diff[:], in1=diff[:], op=ALU.mult)
         dist_sq = keep.tile([P, 2, N], F32)
         nc.vector.tensor_reduce(out=dist_sq[:], in_=diff[:], axis=mybir.AxisListType.X, op=ALU.add)
@@ -142,6 +165,7 @@ def tile_edgefeaturenet_pa_t_kernel(
             nc.vector.tensor_tensor(out=dist_sq[:], in0=dist_sq[:], in1=on_edge[:], op=ALU.add)
 
         emb_t_of = {}
+        steps_of = {}
         grouped_of = {}
         codes_of = {}
 
@@ -155,8 +179,12 @@ def tile_edgefeaturenet_pa_t_kernel(
             nc.scalar.copy(out=emb_t[:], in_=emb_t_ps[:])
             emb_t_of[batch] = emb_t
 
-        def pair_features(batch):
+        def node_features(batch):
             js = slice(batch * JB, (batch + 1) * JB)
+            pm = pm_ring[batch % PM_RING]
+            nc.scalar.copy(out=pm[:, :, HID : 2 * HID], in_=n2e_j[:, js, :])
+
+        def embedding_features(batch):
             pm = pm_ring[batch % PM_RING]
             emb_t = emb_t_of[batch]
             rel_ps = ps_rel.tile([P, JB, HID], F32)
@@ -168,7 +196,9 @@ def tile_edgefeaturenet_pa_t_kernel(
                     out=rel_ps[:, a, :], lhsT=emb_t[:, a, :], rhs=wrp[:], start=False, stop=True
                 )
             nc.scalar.copy(out=pm[:, :, 2 * HID : 3 * HID], in_=rel_ps[:])
-            nc.scalar.copy(out=pm[:, :, HID : 2 * HID], in_=n2e_j[:, js, :])
+
+        def compare(batch):
+            js = slice(batch * JB, (batch + 1) * JB)
             steps = work.tile([P, 2, JB, NB + 1], BF16)
             nc.vector.tensor_tensor(
                 out=steps[:],
@@ -176,13 +206,30 @@ def tile_edgefeaturenet_pa_t_kernel(
                 in1=step_at[:].unsqueeze(1).unsqueeze(1).to_broadcast([P, 2, JB, NB + 1]),
                 op=ALU.is_gt,
             )
-            nc.gpsimd.tensor_tensor(
+            steps_of[batch] = steps
+
+        def bins(batch, small):
+            pm = pm_ring[batch % PM_RING]
+            steps = steps_of[batch]
+            small.tensor_tensor(
                 out=pm[:, :, 3 * HID : 3 * HID + 2 * NB].rearrange("p a (g k) -> p a g k", g=2),
                 in0=steps[:, :, :, 0:NB].rearrange("p g a k -> p a g k"),
                 in1=steps[:, :, :, 1 : NB + 1].rearrange("p g a k -> p a g k"),
                 op=ALU.subtract,
             )
-            nc.gpsimd.tensor_copy(out=pm[:, :, F - 1 : F], in_=flow_j[:, js].unsqueeze(2))
+
+        def flag(batch, small):
+            js = slice(batch * JB, (batch + 1) * JB)
+            small.tensor_copy(
+                out=pm_ring[batch % PM_RING][:, :, F - 1 : F], in_=flow_j[:, js].unsqueeze(2)
+            )
+
+        def pair_features(batch):
+            embedding_features(batch)
+            node_features(batch)
+            compare(batch)
+            bins(batch, nc.gpsimd)
+            flag(batch, nc.gpsimd)
 
         def features_to_partitions(batch):
             pm_words = pm_ring[batch % PM_RING][:].rearrange("p a k -> p (a k)").bitcast(F32)
@@ -234,7 +281,7 @@ def tile_edgefeaturenet_pa_t_kernel(
                     )
                     nc.vector.tensor_tensor(
                         out=result[:, a, e0 : e0 + BANK], in0=acc[:],
-                        in1=b1_rows[:, e0 : e0 + BANK], op=ALU.add,
+                        in1=b1_bf[:, e0 : e0 + BANK], op=ALU.add,
                     )
             nc.scalar.activation(out=result[:, 0, :], in_=result[:, 0, :], func=ACT.Relu)
             nc.gpsimd.tensor_scalar(
@@ -245,41 +292,56 @@ def tile_edgefeaturenet_pa_t_kernel(
             nc.sync.dma_start(out=out_rows[:, j0 : j0 + JS, :], in_=result[:])
 
         transpose_emb(0)
-        pair_features(0)
-        transpose_emb(1)
+        compare(0)
+        bins(0, nc.vector)
+        compare(1)
+        embedding_features(0)
+        constant_node_features(0)
+        node_features(0)
+        constant_flag(0, nc.vector)
+        flag(0, nc.vector)
+        features_to_partitions(0)
         w1_grouped = keep.tile([P, E, PACK], BF16, align_bytes=64)
         w1_codes = keep.tile([P, E], U32, align_bytes=64)
         w1_scales = keep.tile([P, E], U8, align_bytes=64)
-        nc.vector.tensor_copy(
-            out=w1_grouped[:, 0:BANK, :], in_=w1_raw[:, :, 0:BANK].rearrange("p t e -> p e t")
-        )
-        nc.scalar.copy(
-            out=w1_grouped[:, BANK:E, :], in_=w1_raw[:, :, BANK:E].rearrange("p t e -> p e t")
-        )
-        pair_features(1)
-        transpose_emb(2)
-        features_to_partitions(0)
+        for e0 in range(0, E, BANK):
+            nc.vector.tensor_copy(
+                out=w1_grouped[:, e0 : e0 + BANK, :],
+                in_=w1_raw[:, :, e0 : e0 + BANK].rearrange("p t e -> p e t"),
+            )
         for e0 in range(0, E, BANK):
             nc.vector.quantize_mx(
                 out=w1_codes[:, e0 : e0 + BANK].bitcast(FP8X4),
                 scales=w1_scales[:, e0 : e0 + BANK],
                 in_=w1_grouped[:, e0 : e0 + BANK, :].rearrange("p e t -> p (e t)"),
             )
-        b1_rows = keep.tile([P, E], F32)
-        nc.scalar.copy(out=b1_rows[:], in_=b1_bf[:])
-        pair_features(2)
-        transpose_emb(3)
+        constant_flag(1, nc.gpsimd)
+        bins(1, nc.gpsimd)
+        flag(1, nc.gpsimd)
         quantise(0)
-        features_to_partitions(1)
+        transpose_emb(1)
+        constant_node_features(1)
+        node_features(1)
+        embedding_features(1)
+        transpose_emb(2)
 
         for batch in range(BATCHES):
             multiply(batch, 0)
+            if batch == 0:
+                features_to_partitions(1)
+                constant_node_features(2)
+                constant_flag(2, nc.gpsimd)
+                pair_features(2)
+                transpose_emb(3)
+                quantise(1)
+                multiply(batch, JS)
             if batch + 3 < BATCHES:
                 pair_features(batch + 3)
             if batch + 4 < BATCHES:
                 transpose_emb(batch + 4)
-            if batch + 1 < BATCHES:
-                quantise(batch + 1)
-            multiply(batch, JS)
+            if batch > 0:
+                if batch + 1 < BATCHES:
+                    quantise(batch + 1)
+                multiply(batch, JS)
             if batch + 2 < BATCHES:
                 features_to_partitions(batch + 2)

@@ -165,6 +165,7 @@ def tile_edgefeaturenet_pa_t_kernel(
             nc.vector.tensor_tensor(out=dist_sq[:], in0=dist_sq[:], in1=on_edge[:], op=ALU.add)
 
         emb_t_of = {}
+        steps_all = keep.tile([P, BATCHES, 2, JB, NB + 1], BF16)
         steps_of = {}
         grouped_of = {}
         codes_of = {}
@@ -199,9 +200,9 @@ def tile_edgefeaturenet_pa_t_kernel(
 
         def compare(batch):
             js = slice(batch * JB, (batch + 1) * JB)
-            steps = work.tile([P, 2, JB, NB + 1], BF16)
+            steps = steps_all[:, batch, :, :, :]
             nc.vector.tensor_tensor(
-                out=steps[:],
+                out=steps,
                 in0=dist_sq[:, :, js].unsqueeze(3).to_broadcast([P, 2, JB, NB + 1]),
                 in1=step_at[:].unsqueeze(1).unsqueeze(1).to_broadcast([P, 2, JB, NB + 1]),
                 op=ALU.is_gt,
@@ -227,7 +228,8 @@ def tile_edgefeaturenet_pa_t_kernel(
         def pair_features(batch):
             embedding_features(batch)
             node_features(batch)
-            compare(batch)
+            if batch not in steps_of:
+                compare(batch)
             bins(batch, nc.gpsimd)
             flag(batch, nc.gpsimd)
 
@@ -295,6 +297,8 @@ def tile_edgefeaturenet_pa_t_kernel(
         compare(0)
         bins(0, nc.vector)
         compare(1)
+        for ahead in [2,3,4]:
+            compare(ahead)
         embedding_features(0)
         constant_node_features(0)
         node_features(0)
@@ -319,6 +323,8 @@ def tile_edgefeaturenet_pa_t_kernel(
         bins(1, nc.gpsimd)
         flag(1, nc.gpsimd)
         quantise(0)
+        for ahead in [5,6,7,8,9,10]:
+            compare(ahead)
         transpose_emb(1)
         constant_node_features(1)
         node_features(1)
@@ -333,6 +339,8 @@ def tile_edgefeaturenet_pa_t_kernel(
                 constant_flag(2, nc.gpsimd)
                 pair_features(2)
                 transpose_emb(3)
+                for ahead in [11,12,13,14,15]:
+                    compare(ahead)
                 quantise(1)
                 multiply(batch, JS)
             if batch + 3 < BATCHES:

@@ -265,8 +265,17 @@ def tile_edgefeaturenet_pa_t_kernel(
             )
             codes_of[batch] = (codes, scales)
 
+        def relu_on_scalar(values):
+            nc.scalar.activation(out=values, in_=values, func=ACT.Relu)
+
+        def relu_on_gpsimd(values):
+            nc.gpsimd.tensor_scalar(
+                out=values, in0=values, scalar1=float("inf"), scalar2=0.0, op0=ALU.min, op1=ALU.max
+            )
+
         def multiply(batch, a0):
             codes, scales = codes_of[batch]
+            last = batch == BATCHES - 1 and a0 == JB - JS
             result = stores.tile([P, JS, E], F32)
             for a in range(JS):
                 pairs = slice((a0 + a) * P, (a0 + a + 1) * P)
@@ -285,18 +294,25 @@ def tile_edgefeaturenet_pa_t_kernel(
                         out=result[:, a, e0 : e0 + BANK], in0=acc[:],
                         in1=b1_bf[:, e0 : e0 + BANK], op=ALU.add,
                     )
-            nc.scalar.activation(out=result[:, 0, :], in_=result[:, 0, :], func=ACT.Relu)
-            nc.gpsimd.tensor_scalar(
-                out=result[:, 1, :], in0=result[:, 1, :],
-                scalar1=float("inf"), scalar2=0.0, op0=ALU.min, op1=ALU.max,
-            )
             j0 = batch * JB + a0
-            nc.sync.dma_start(out=out_rows[:, j0 : j0 + JS, :], in_=result[:])
+            if last:
+                relu_on_scalar(result[:, 0, 0:BANK])
+                relu_on_gpsimd(result[:, 0, BANK:E])
+                nc.sync.dma_start(out=out_rows[:, j0, :], in_=result[:, 0, :])
+                relu_on_scalar(result[:, 1, 0:BANK])
+                nc.vector.tensor_scalar_max(
+                    out=result[:, 1, BANK:E], in0=result[:, 1, BANK:E], scalar1=0.0
+                )
+                nc.sync.dma_start(out=out_rows[:, j0 + 1, :], in_=result[:, 1, :])
+            else:
+                relu_on_scalar(result[:, 0, :])
+                relu_on_gpsimd(result[:, 1, :])
+                nc.sync.dma_start(out=out_rows[:, j0 : j0 + JS, :], in_=result[:])
 
         transpose_emb(0)
         compare(0)
-        bins(0, nc.vector)
         compare(1)
+        bins(0, nc.vector)
         for ahead in [2,3,4]:
             compare(ahead)
         embedding_features(0)
@@ -310,8 +326,8 @@ def tile_edgefeaturenet_pa_t_kernel(
         w1_scales = keep.tile([P, E], U8, align_bytes=64)
         for e0 in range(0, E, BANK):
             nc.vector.tensor_copy(
-                out=w1_grouped[:, e0 : e0 + BANK, :],
-                in_=w1_raw[:, :, e0 : e0 + BANK].rearrange("p t e -> p e t"),
+                out=w1_grouped[:, e0 : e0 + BANK, :].rearrange("p (c i) t -> p c t i", i=PACK),
+                in_=w1_raw[:, :, e0 : e0 + BANK].rearrange("p t (c i) -> p c t i", i=PACK),
             )
         for e0 in range(0, E, BANK):
             nc.vector.quantize_mx(

@@ -54,11 +54,9 @@ def tile_edgefeaturenet_pa_t_kernel(
         ctx.enter_context(tc.manual_schedule())
         keep = ctx.enter_context(tc.tile_pool(name="keep", bufs=1))
         work = ctx.enter_context(tc.tile_pool(name="work", bufs=2))
-        stores = ctx.enter_context(tc.tile_pool(name="stores", bufs=4))
-        ps_emb = ctx.enter_context(tc.psum_pool(name="ps_emb", bufs=1))
-        ps_rel = ctx.enter_context(tc.psum_pool(name="ps_rel", bufs=1))
-        ps_feat = ctx.enter_context(tc.psum_pool(name="ps_feat", bufs=2))
-        ps_acc = ctx.enter_context(tc.psum_pool(name="ps_acc", bufs=4))
+        stores = ctx.enter_context(tc.tile_pool(name="stores", bufs=6))
+        ps_plain = ctx.enter_context(tc.psum_pool(name="ps_plain", bufs=2))
+        ps_acc = ctx.enter_context(tc.psum_pool(name="ps_acc", bufs=6))
 
         emb = keep.tile([P, N, HID], BF16)
         n2e_j = keep.tile([P, N, HID], BF16)
@@ -171,7 +169,7 @@ def tile_edgefeaturenet_pa_t_kernel(
         codes_of = {}
 
         def transpose_emb(batch):
-            emb_t_ps = ps_emb.tile([P, JB, P], BF16)
+            emb_t_ps = ps_plain.tile([P, JB, P], BF16, name="plain_bank")
             for a in range(JB):
                 nc.tensor.transpose(
                     out=emb_t_ps[:, a, :], in_=emb[:, batch * JB + a, :], identity=ident[:]
@@ -188,7 +186,7 @@ def tile_edgefeaturenet_pa_t_kernel(
         def embedding_features(batch):
             pm = pm_ring[batch % PM_RING]
             emb_t = emb_t_of[batch]
-            rel_ps = ps_rel.tile([P, JB, HID], F32)
+            rel_ps = ps_plain.tile([P, JB, HID], F32, name="plain_bank")
             for a in range(JB):
                 nc.tensor.matmul(
                     out=rel_ps[:, a, :], lhsT=ones_row[:], rhs=brp_row[:], start=True, stop=False
@@ -225,11 +223,7 @@ def tile_edgefeaturenet_pa_t_kernel(
                 out=pm_ring[batch % PM_RING][:, :, F - 1 : F], in_=flow_j[:, js].unsqueeze(2)
             )
 
-        def pair_features(batch):
-            embedding_features(batch)
-            node_features(batch)
-            if batch not in steps_of:
-                compare(batch)
+        def other_features(batch):
             bins(batch, nc.gpsimd)
             flag(batch, nc.gpsimd)
 
@@ -238,7 +232,7 @@ def tile_edgefeaturenet_pa_t_kernel(
             grouped = work.tile([P, JB, P, PACK], BF16, align_bytes=64)
             grouped_words = grouped[:].rearrange("p a n t -> p (a n t)").bitcast(F32)
             for a0 in range(0, JB, 2):
-                feat_ps = ps_feat.tile([P, 2, 2, P], F32)
+                feat_ps = ps_plain.tile([P, 2, 2, P], F32, name="plain_bank")
                 for a in range(2):
                     for u in range(2):
                         w0 = (a0 + a) * 2 * P
@@ -273,9 +267,10 @@ def tile_edgefeaturenet_pa_t_kernel(
                 out=values, in0=values, scalar1=float("inf"), scalar2=0.0, op0=ALU.min, op1=ALU.max
             )
 
+        result_of = {}
+
         def multiply(batch, a0):
             codes, scales = codes_of[batch]
-            last = batch == BATCHES - 1 and a0 == JB - JS
             result = stores.tile([P, JS, E], F32)
             for a in range(JS):
                 pairs = slice((a0 + a) * P, (a0 + a + 1) * P)
@@ -294,6 +289,11 @@ def tile_edgefeaturenet_pa_t_kernel(
                         out=result[:, a, e0 : e0 + BANK], in0=acc[:],
                         in1=b1_bf[:, e0 : e0 + BANK], op=ALU.add,
                     )
+            result_of[batch, a0] = result
+
+        def finish(batch, a0):
+            result = result_of[batch, a0]
+            last = batch == BATCHES - 1 and a0 == JB - JS
             j0 = batch * JB + a0
             if last:
                 relu_on_scalar(result[:, 0, 0:BANK])
@@ -353,19 +353,28 @@ def tile_edgefeaturenet_pa_t_kernel(
                 features_to_partitions(1)
                 constant_node_features(2)
                 constant_flag(2, nc.gpsimd)
-                pair_features(2)
+                node_features(2)
+                embedding_features(2)
                 transpose_emb(3)
+                finish(batch, 0)
+                other_features(2)
                 for ahead in [11,12,13,14,15]:
                     compare(ahead)
                 quantise(1)
                 multiply(batch, JS)
             if batch + 3 < BATCHES:
-                pair_features(batch + 3)
+                node_features(batch + 3)
+                embedding_features(batch + 3)
             if batch + 4 < BATCHES:
                 transpose_emb(batch + 4)
+            if batch > 0:
+                finish(batch, 0)
+            if batch + 3 < BATCHES:
+                other_features(batch + 3)
             if batch > 0:
                 if batch + 1 < BATCHES:
                     quantise(batch + 1)
                 multiply(batch, JS)
             if batch + 2 < BATCHES:
                 features_to_partitions(batch + 2)
+            finish(batch, JS)

@@ -86,7 +86,19 @@ def tile_edgefeaturenet_pa_t_kernel(
         nc.vector.memset(brp_row[:], 0.0)
         nc.sync.dma_start(out=brp_row[0:1, :], in_=b_rp.unsqueeze(0))
         w1_raw = keep.tile([P, PACK, E], BF16)
-        nc.sync.dma_start(out=w1_raw[:], in_=W1.rearrange("(p t) e -> p t e", t=PACK))
+        nc.sync.dma_start(
+            out=w1_raw[0:64, :, :].rearrange("p (u e) c -> p u (e c)", u=2),
+            in_=W1[0 : 2 * HID, :].rearrange("(u p e) c -> p u (e c)", u=2, e=2),
+        )
+        nc.sync.dma_start(
+            out=w1_raw[64:96, :, :],
+            in_=W1[2 * HID : 3 * HID, :].rearrange("(p t) c -> p t c", t=PACK),
+        )
+        for g in range(2):
+            nc.sync.dma_start(
+                out=w1_raw[96:128, 2 * g : 2 * g + 2, :],
+                in_=W1[3 * HID + g * NB : 3 * HID + g * NB + 64, :].rearrange("(p e) c -> p e c", e=2),
+            )
         n2e_i = keep.tile([P, HID], BF16)
         nc.sync.dma_start(out=n2e_i[:], in_=n2e.rearrange("b i h -> (b i) h"))
         load_nodes(slice(0, JB))
@@ -97,6 +109,7 @@ def tile_edgefeaturenet_pa_t_kernel(
             out=flow_all[:].rearrange("p b j -> p (b j)"),
             in_=flow_mask.rearrange("b j -> (b j)").partition_broadcast(P),
         )
+        nc.sync.dma_start(out=w1_raw[127:128, 1, :], in_=W1[F - 1 : F, :])
         b1_bf = keep.tile([P, E], BF16)
         nc.sync.dma_start(out=b1_bf[:], in_=b1.partition_broadcast(P))
         for first in range(JB, N, JL):
@@ -107,6 +120,13 @@ def tile_edgefeaturenet_pa_t_kernel(
         make_identity(nc, ident[:])
         ident_words = keep.tile([P, P], F32)
         make_identity(nc, ident_words[:])
+        wrp_words = keep.tile([P, HID], BF16)
+        brp_words = keep.tile([P, HID], BF16)
+        for source, ordered in ((wrp, wrp_words), (brp_row, brp_words)):
+            nc.gpsimd.tensor_copy(
+                out=ordered[:].rearrange("p (u w e) -> p u w e", u=2, e=2),
+                in_=source[:].rearrange("p (w u e) -> p u w e", u=2, e=2),
+            )
         ones_row = keep.tile([P, P], BF16)
         nc.vector.memset(ones_row[:], 0.0)
         nc.vector.memset(ones_row[0:1, :], 1.0)
@@ -131,6 +151,9 @@ def tile_edgefeaturenet_pa_t_kernel(
             pm = keep.tile([P, JB, F], BF16, name="pm%d" % ring)
             pm_ring.append(pm)
 
+        def halves(pm):
+            return pm[:].rearrange("p a (u k) -> p a u k", u=2)
+
         def constant_node_features(ring):
             nc.scalar.copy(
                 out=pm_ring[ring][:, :, 0:HID], in_=n2e_i[:].unsqueeze(1).to_broadcast([P, JB, HID])
@@ -138,7 +161,7 @@ def tile_edgefeaturenet_pa_t_kernel(
 
         def constant_flag(ring, small):
             small.tensor_copy(
-                out=pm_ring[ring][:, :, F - 2 : F - 1],
+                out=pm_ring[ring][:, :, F - 1 : F],
                 in_=flow_i[:].unsqueeze(1).to_broadcast([P, JB, 1]),
             )
 
@@ -181,7 +204,7 @@ def tile_edgefeaturenet_pa_t_kernel(
         def node_features(batch):
             js = slice(batch * JB, (batch + 1) * JB)
             pm = pm_ring[batch % PM_RING]
-            nc.scalar.copy(out=pm[:, :, HID : 2 * HID], in_=n2e_j[:, js, :])
+            nc.scalar.copy(out=halves(pm)[:, :, 1, 0:HID], in_=n2e_j[:, js, :])
 
         def embedding_features(batch):
             pm = pm_ring[batch % PM_RING]
@@ -189,12 +212,15 @@ def tile_edgefeaturenet_pa_t_kernel(
             rel_ps = ps_plain.tile([P, JB, HID], F32, name="plain_bank")
             for a in range(JB):
                 nc.tensor.matmul(
-                    out=rel_ps[:, a, :], lhsT=ones_row[:], rhs=brp_row[:], start=True, stop=False
+                    out=rel_ps[:, a, :], lhsT=ones_row[:], rhs=brp_words[:], start=True, stop=False
                 )
                 nc.tensor.matmul(
-                    out=rel_ps[:, a, :], lhsT=emb_t[:, a, :], rhs=wrp[:], start=False, stop=True
+                    out=rel_ps[:, a, :], lhsT=emb_t[:, a, :], rhs=wrp_words[:], start=False, stop=True
                 )
-            nc.scalar.copy(out=pm[:, :, 2 * HID : 3 * HID], in_=rel_ps[:])
+            nc.scalar.copy(
+                out=halves(pm)[:, :, :, HID : HID + 64],
+                in_=rel_ps[:].rearrange("p a (u k) -> p a u k", u=2),
+            )
 
         def compare(batch):
             js = slice(batch * JB, (batch + 1) * JB)
@@ -211,7 +237,7 @@ def tile_edgefeaturenet_pa_t_kernel(
             pm = pm_ring[batch % PM_RING]
             steps = steps_of[batch]
             small.tensor_tensor(
-                out=pm[:, :, 3 * HID : 3 * HID + 2 * NB].rearrange("p a (g k) -> p a g k", g=2),
+                out=halves(pm)[:, :, :, HID + 64 : HID + 64 + NB],
                 in0=steps[:, :, :, 0:NB].rearrange("p g a k -> p a g k"),
                 in1=steps[:, :, :, 1 : NB + 1].rearrange("p g a k -> p a g k"),
                 op=ALU.subtract,
@@ -220,7 +246,7 @@ def tile_edgefeaturenet_pa_t_kernel(
         def flag(batch, small):
             js = slice(batch * JB, (batch + 1) * JB)
             small.tensor_copy(
-                out=pm_ring[batch % PM_RING][:, :, F - 1 : F], in_=flow_j[:, js].unsqueeze(2)
+                out=pm_ring[batch % PM_RING][:, :, F // 2 - 1 : F // 2], in_=flow_j[:, js].unsqueeze(2)
             )
 
         def other_features(batch):
@@ -235,9 +261,9 @@ def tile_edgefeaturenet_pa_t_kernel(
                 feat_ps = ps_plain.tile([P, 2, 2, P], F32, name="plain_bank")
                 for a in range(2):
                     for u in range(2):
-                        w0 = (a0 + a) * 2 * P
+                        w0 = ((a0 + a) * 2 + u) * P
                         nc.tensor.transpose(
-                            out=feat_ps[:, a, u, :], in_=pm_words[:, w0 + u : w0 + 2 * P : 2],
+                            out=feat_ps[:, a, u, :], in_=pm_words[:, w0 : w0 + P],
                             identity=ident_words[:],
                         )
                 nc.scalar.copy(

@@ -6,6 +6,7 @@ from concourse.masks import make_identity
 F32 = mybir.dt.float32
 BF16 = mybir.dt.bfloat16
 U32 = mybir.dt.uint32
+I32 = mybir.dt.int32
 U8 = mybir.dt.uint8
 FP8X4 = mybir.dt.float8_e4m3fn_x4
 ALU = mybir.AluOpType
@@ -21,26 +22,15 @@ BANK = 512
 JB = 4
 JS = 2
 JL = (N - JB) // 3
-PM_RING = 3
-EDGES_ON_VECTOR = 40
+HALF = F // 2
+EDGE = HID + 64
 BATCHES = N // JB
 
 FLOPS = 2 * B * N * N * F * E + 2 * B * N * N * HID * HID
 
 
-def floor_to_float32(x):
-    mantissa, exponent = x, 0
-    while mantissa >= 2.0:
-        mantissa, exponent = mantissa / 2.0, exponent + 1
-    while mantissa < 1.0:
-        mantissa, exponent = mantissa * 2.0, exponent - 1
-    return int(mantissa * 2.0**23) / 2.0**23 * 2.0**exponent
-
-
-EDGES = [k * ((MAX_BIN - MIN_BIN) / (NB - 1)) + MIN_BIN for k in range(NB - 1)] + [MAX_BIN, FAR]
-EDGES_SQ = [edge * edge for edge in EDGES]
-STEP_AT = [floor_to_float32(sq) for sq in EDGES_SQ]
-ON_EDGE = [sq for sq in EDGES_SQ if floor_to_float32(sq) == sq]
+BIN = (MAX_BIN - MIN_BIN) / (NB - 1)
+BIN_HIGH = 41.0 / 128.0
 
 
 def tile_edgefeaturenet_pa_t_kernel(
@@ -59,7 +49,8 @@ def tile_edgefeaturenet_pa_t_kernel(
         ps_acc = ctx.enter_context(tc.psum_pool(name="ps_acc", bufs=6))
 
         emb = keep.tile([P, N, HID], BF16)
-        n2e_j = keep.tile([P, N, HID], BF16)
+        pm = keep.tile([P, N, F], BF16)
+        halves = pm[:].rearrange("p j (u k) -> p j u k", u=2)
 
         def load_emb(js):
             nc.sync.dma_start(out=emb[:, js, :], in_=emb_rows[:, js, :])
@@ -67,19 +58,26 @@ def tile_edgefeaturenet_pa_t_kernel(
         def load_nodes(js):
             for b in range(B):
                 nc.sync.dma_start(
-                    out=n2e_j[b * N : (b + 1) * N, js, :].rearrange("p j h -> p (j h)"),
-                    in_=n2e[b, js, :].rearrange("j h -> (j h)").partition_broadcast(N),
+                    out=pm[b * N : (b + 1) * N, js, HALF : HALF + HID],
+                    in_=n2e[b, js, :].partition_broadcast(N),
                 )
 
         load_emb(slice(0, JB))
         pos_all = keep.tile([P, 2, B, N, XYZ], BF16)
         posi = keep.tile([P, 2, 16], BF16)
         for g, pos in enumerate((trans, sc_trans)):
-            nc.sync.dma_start(
+            nc.scalar.dma_start(
                 out=pos_all[:, g, :, :, :].rearrange("p b j c -> p (b j c)"),
                 in_=pos.rearrange("b j c -> (b j c)").partition_broadcast(P),
             )
-            nc.sync.dma_start(out=posi[:, g, 0:XYZ], in_=pos.rearrange("b i c -> (b i) c"))
+            nc.scalar.dma_start(out=posi[:, g, 0:XYZ], in_=pos.rearrange("b i c -> (b i) c"))
+        flow_i = keep.tile([P, 1], BF16)
+        nc.scalar.dma_start(out=flow_i[:], in_=flow_mask.rearrange("b i -> (b i)").unsqueeze(1))
+        flow_all = keep.tile([P, B, N], BF16)
+        nc.scalar.dma_start(
+            out=flow_all[:].rearrange("p b j -> p (b j)"),
+            in_=flow_mask.rearrange("b j -> (b j)").partition_broadcast(P),
+        )
         wrp = keep.tile([P, HID], BF16)
         nc.sync.dma_start(out=wrp[:], in_=W_rp)
         brp_row = keep.tile([P, HID], BF16)
@@ -102,13 +100,6 @@ def tile_edgefeaturenet_pa_t_kernel(
         n2e_i = keep.tile([P, HID], BF16)
         nc.sync.dma_start(out=n2e_i[:], in_=n2e.rearrange("b i h -> (b i) h"))
         load_nodes(slice(0, JB))
-        flow_i = keep.tile([P, 1], BF16)
-        nc.sync.dma_start(out=flow_i[:], in_=flow_mask.rearrange("b i -> (b i)").unsqueeze(1))
-        flow_all = keep.tile([P, B, N], BF16)
-        nc.sync.dma_start(
-            out=flow_all[:].rearrange("p b j -> p (b j)"),
-            in_=flow_mask.rearrange("b j -> (b j)").partition_broadcast(P),
-        )
         nc.sync.dma_start(out=w1_raw[127:128, 1, :], in_=W1[F - 1 : F, :])
         b1_bf = keep.tile([P, E], BF16)
         nc.sync.dma_start(out=b1_bf[:], in_=b1.partition_broadcast(P))
@@ -130,40 +121,21 @@ def tile_edgefeaturenet_pa_t_kernel(
         ones_row = keep.tile([P, P], BF16)
         nc.vector.memset(ones_row[:], 0.0)
         nc.vector.memset(ones_row[0:1, :], 1.0)
-        flow_j = keep.tile([P, N], BF16)
+        bin_row = keep.tile([P, 64], BF16)
+        nc.gpsimd.iota(
+            bin_row[:], pattern=[[1, 64]], base=0, channel_multiplier=0,
+            allow_small_or_imprecise_dtypes=True,
+        )
+        flags = keep.tile([P, N, 2], BF16)
         for b in range(B):
-            nc.gpsimd.tensor_copy(
-                out=flow_j[b * N : (b + 1) * N, :], in_=flow_all[b * N : (b + 1) * N, b, :]
-            )
-        step_at = keep.tile([P, NB + 1], F32)
+            rows = slice(b * N, (b + 1) * N)
+            nc.gpsimd.tensor_copy(out=flags[rows, :, 0:1], in_=flow_all[rows, b, :].unsqueeze(2))
+        nc.gpsimd.tensor_copy(
+            out=flags[:, :, 1:2], in_=flow_i[:].unsqueeze(1).to_broadcast([P, N, 1])
+        )
         zero = keep.tile([P, 1], F32)
         nc.vector.memset(zero[:], 0.0)
-        for k in range(NB + 1):
-            if k < EDGES_ON_VECTOR:
-                nc.vector.memset(step_at[:, k : k + 1], STEP_AT[k])
-            else:
-                nc.scalar.activation(
-                    out=step_at[:, k : k + 1], in_=zero[:], func=ACT.Copy, bias=STEP_AT[k], scale=1.0
-                )
-
-        pm_ring = []
-        for ring in range(PM_RING):
-            pm = keep.tile([P, JB, F], BF16, name="pm%d" % ring)
-            pm_ring.append(pm)
-
-        def halves(pm):
-            return pm[:].rearrange("p a (u k) -> p a u k", u=2)
-
-        def constant_node_features(ring):
-            nc.scalar.copy(
-                out=pm_ring[ring][:, :, 0:HID], in_=n2e_i[:].unsqueeze(1).to_broadcast([P, JB, HID])
-            )
-
-        def constant_flag(ring, small):
-            small.tensor_copy(
-                out=pm_ring[ring][:, :, F - 1 : F],
-                in_=flow_i[:].unsqueeze(1).to_broadcast([P, JB, 1]),
-            )
+        nc.scalar.activation(out=zero[:], in_=zero[:], func=ACT.Sqrt)
 
         diff = keep.tile([P, 2, N, XYZ], F32)
         for b in range(B):
@@ -177,17 +149,75 @@ def tile_edgefeaturenet_pa_t_kernel(
         nc.vector.tensor_tensor(out=diff[:], in0=diff[:], in1=diff[:], op=ALU.mult)
         dist_sq = keep.tile([P, 2, N], F32)
         nc.vector.tensor_reduce(out=dist_sq[:], in_=diff[:], axis=mybir.AxisListType.X, op=ALU.add)
+        root = keep.tile([P, 2, N], F32)
+        near = keep.tile([P, 2, N], I32)
+        edge = keep.tile([P, 2, N], F32)
+        edge_low = keep.tile([P, 2, N], F32)
+        edge_sq = keep.tile([P, 2, N], F32)
+        rest = keep.tile([P, 2, N], F32)
+        beyond = keep.tile([P, 2, N], F32)
         on_edge = keep.tile([P, 2, N], F32)
-        for sq in ON_EDGE:
+        bin_of = keep.tile([P, 2, N], F32)
+        bin_pair = keep.tile([P, 2, N, 2], BF16)
+
+        def root_of_distances():
+            nc.scalar.activation(
+                out=root[:], in_=dist_sq[:], func=ACT.Sqrt, scale=1.0 / (BIN * BIN)
+            )
+
+        def bins_of_distances():
             nc.vector.tensor_scalar(
-                out=on_edge[:], in0=dist_sq[:], scalar1=sq, scalar2=-(sq + 1.0),
+                out=near[:], in0=root[:], scalar1=0.25 - MIN_BIN / BIN, scalar2=NB - 1 + 0.3,
+                op0=ALU.add, op1=ALU.min,
+            )
+            nc.vector.tensor_scalar(
+                out=on_edge[:], in0=dist_sq[:], scalar1=MAX_BIN * MAX_BIN, scalar2=0.5,
                 op0=ALU.is_equal, op1=ALU.mult,
             )
-            nc.vector.tensor_tensor(out=dist_sq[:], in0=dist_sq[:], in1=on_edge[:], op=ALU.add)
+            nc.vector.tensor_scalar(
+                out=edge[:], in0=near[:], scalar1=BIN_HIGH, scalar2=0.0, op0=ALU.mult, op1=ALU.add
+            )
+            nc.vector.tensor_scalar(
+                out=edge_low[:], in0=near[:], scalar1=BIN - BIN_HIGH, scalar2=MIN_BIN,
+                op0=ALU.mult, op1=ALU.add,
+            )
+            nc.vector.scalar_tensor_tensor(
+                out=on_edge[:], in0=dist_sq[:], scalar=FAR * FAR, in1=on_edge[:],
+                op0=ALU.is_ge, op1=ALU.add,
+            )
+            nc.vector.tensor_tensor(out=edge_sq[:], in0=edge[:], in1=edge[:], op=ALU.mult)
+            nc.vector.scalar_tensor_tensor(
+                out=rest[:], in0=edge[:], scalar=2.0, in1=edge_low[:], op0=ALU.mult, op1=ALU.add
+            )
+            nc.vector.tensor_tensor(out=edge_sq[:], in0=dist_sq[:], in1=edge_sq[:], op=ALU.subtract)
+            nc.vector.tensor_tensor(out=rest[:], in0=rest[:], in1=edge_low[:], op=ALU.mult)
+            nc.vector.scalar_tensor_tensor(
+                out=on_edge[:], in0=near[:], scalar=-1.0, in1=on_edge[:], op0=ALU.add, op1=ALU.add
+            )
+            nc.vector.tensor_tensor(out=beyond[:], in0=edge_sq[:], in1=rest[:], op=ALU.is_gt)
+            nc.vector.tensor_tensor(
+                out=bin_pair[:],
+                in0=beyond[:].unsqueeze(3).to_broadcast([P, 2, N, 2]),
+                in1=on_edge[:].unsqueeze(3).to_broadcast([P, 2, N, 2]),
+                op=ALU.add,
+            )
+
+        def distograms(js):
+            count = js.stop - js.start
+            for g in range(2):
+                nc.vector.tensor_tensor(
+                    out=halves[:, js, g, EDGE:HALF].rearrange("p j (w e) -> p j w e", e=2),
+                    in0=bin_pair[:, g, js, :].unsqueeze(2).to_broadcast([P, count, 32, 2]),
+                    in1=bin_row[:].rearrange("p (w e) -> p w e", e=2).unsqueeze(1).to_broadcast(
+                        [P, count, 32, 2]
+                    ),
+                    op=ALU.is_equal,
+                )
+            nc.vector.tensor_copy(
+                out=halves[:, js, :, HALF - 1 : HALF], in_=flags[:, js, :].unsqueeze(3)
+            )
 
         emb_t_of = {}
-        steps_all = keep.tile([P, BATCHES, 2, JB, NB + 1], BF16)
-        steps_of = {}
         grouped_of = {}
         codes_of = {}
 
@@ -203,11 +233,12 @@ def tile_edgefeaturenet_pa_t_kernel(
 
         def node_features(batch):
             js = slice(batch * JB, (batch + 1) * JB)
-            pm = pm_ring[batch % PM_RING]
-            nc.scalar.copy(out=halves(pm)[:, :, 1, 0:HID], in_=n2e_j[:, js, :])
+            nc.scalar.copy(
+                out=pm[:, js, 0:HID], in_=n2e_i[:].unsqueeze(1).to_broadcast([P, JB, HID])
+            )
 
         def embedding_features(batch):
-            pm = pm_ring[batch % PM_RING]
+            js = slice(batch * JB, (batch + 1) * JB)
             emb_t = emb_t_of[batch]
             rel_ps = ps_plain.tile([P, JB, HID], F32, name="plain_bank")
             for a in range(JB):
@@ -218,43 +249,12 @@ def tile_edgefeaturenet_pa_t_kernel(
                     out=rel_ps[:, a, :], lhsT=emb_t[:, a, :], rhs=wrp_words[:], start=False, stop=True
                 )
             nc.scalar.copy(
-                out=halves(pm)[:, :, :, HID : HID + 64],
+                out=halves[:, js, :, HID:EDGE],
                 in_=rel_ps[:].rearrange("p a (u k) -> p a u k", u=2),
             )
 
-        def compare(batch):
-            js = slice(batch * JB, (batch + 1) * JB)
-            steps = steps_all[:, batch, :, :, :]
-            nc.vector.tensor_tensor(
-                out=steps,
-                in0=dist_sq[:, :, js].unsqueeze(3).to_broadcast([P, 2, JB, NB + 1]),
-                in1=step_at[:].unsqueeze(1).unsqueeze(1).to_broadcast([P, 2, JB, NB + 1]),
-                op=ALU.is_gt,
-            )
-            steps_of[batch] = steps
-
-        def bins(batch, small):
-            pm = pm_ring[batch % PM_RING]
-            steps = steps_of[batch]
-            small.tensor_tensor(
-                out=halves(pm)[:, :, :, HID + 64 : HID + 64 + NB],
-                in0=steps[:, :, :, 0:NB].rearrange("p g a k -> p a g k"),
-                in1=steps[:, :, :, 1 : NB + 1].rearrange("p g a k -> p a g k"),
-                op=ALU.subtract,
-            )
-
-        def flag(batch, small):
-            js = slice(batch * JB, (batch + 1) * JB)
-            small.tensor_copy(
-                out=pm_ring[batch % PM_RING][:, :, F // 2 - 1 : F // 2], in_=flow_j[:, js].unsqueeze(2)
-            )
-
-        def other_features(batch):
-            bins(batch, nc.gpsimd)
-            flag(batch, nc.gpsimd)
-
         def features_to_partitions(batch):
-            pm_words = pm_ring[batch % PM_RING][:].rearrange("p a k -> p (a k)").bitcast(F32)
+            pm_words = pm[:, batch * JB : (batch + 1) * JB, :].rearrange("p a k -> p (a k)").bitcast(F32)
             grouped = work.tile([P, JB, P, PACK], BF16, align_bytes=64)
             grouped_words = grouped[:].rearrange("p a n t -> p (a n t)").bitcast(F32)
             for a0 in range(0, JB, 2):
@@ -322,8 +322,7 @@ def tile_edgefeaturenet_pa_t_kernel(
             last = batch == BATCHES - 1 and a0 == JB - JS
             j0 = batch * JB + a0
             if last:
-                relu_on_scalar(result[:, 0, 0:BANK])
-                relu_on_gpsimd(result[:, 0, BANK:E])
+                relu_on_scalar(result[:, 0, :])
                 nc.sync.dma_start(out=out_rows[:, j0, :], in_=result[:, 0, :])
                 relu_on_scalar(result[:, 1, 0:BANK])
                 nc.vector.tensor_scalar_max(
@@ -336,16 +335,11 @@ def tile_edgefeaturenet_pa_t_kernel(
                 nc.sync.dma_start(out=out_rows[:, j0 : j0 + JS, :], in_=result[:])
 
         transpose_emb(0)
-        compare(0)
-        compare(1)
-        bins(0, nc.vector)
-        for ahead in [2,3,4]:
-            compare(ahead)
+        root_of_distances()
+        bins_of_distances()
+        distograms(slice(0, JB))
         embedding_features(0)
-        constant_node_features(0)
         node_features(0)
-        constant_flag(0, nc.vector)
-        flag(0, nc.vector)
         features_to_partitions(0)
         w1_grouped = keep.tile([P, E, PACK], BF16, align_bytes=64)
         w1_codes = keep.tile([P, E], U32, align_bytes=64)
@@ -361,14 +355,9 @@ def tile_edgefeaturenet_pa_t_kernel(
                 scales=w1_scales[:, e0 : e0 + BANK],
                 in_=w1_grouped[:, e0 : e0 + BANK, :].rearrange("p e t -> p (e t)"),
             )
-        constant_flag(1, nc.gpsimd)
-        bins(1, nc.gpsimd)
-        flag(1, nc.gpsimd)
         quantise(0)
-        for ahead in [5,6,7,8,9,10]:
-            compare(ahead)
+        distograms(slice(JB, 4 * JB))
         transpose_emb(1)
-        constant_node_features(1)
         node_features(1)
         embedding_features(1)
         transpose_emb(2)
@@ -377,17 +366,14 @@ def tile_edgefeaturenet_pa_t_kernel(
             multiply(batch, 0)
             if batch == 0:
                 features_to_partitions(1)
-                constant_node_features(2)
-                constant_flag(2, nc.gpsimd)
                 node_features(2)
                 embedding_features(2)
                 transpose_emb(3)
                 finish(batch, 0)
-                other_features(2)
-                for ahead in [11,12,13,14,15]:
-                    compare(ahead)
+                distograms(slice(4 * JB, 10 * JB))
                 quantise(1)
                 multiply(batch, JS)
+                distograms(slice(10 * JB, N))
             if batch + 3 < BATCHES:
                 node_features(batch + 3)
                 embedding_features(batch + 3)
@@ -395,9 +381,6 @@ def tile_edgefeaturenet_pa_t_kernel(
                 transpose_emb(batch + 4)
             if batch > 0:
                 finish(batch, 0)
-            if batch + 3 < BATCHES:
-                other_features(batch + 3)
-            if batch > 0:
                 if batch + 1 < BATCHES:
                     quantise(batch + 1)
                 multiply(batch, JS)

@@ -21,6 +21,7 @@ PACK = 4
 BANK = 512
 JB = 4
 JS = 2
+EP = E - P
 JL = (N - JB) // 3
 HALF = F // 2
 EDGE = HID + 64
@@ -44,7 +45,7 @@ def tile_edgefeaturenet_pa_t_kernel(
         ctx.enter_context(tc.manual_schedule())
         keep = ctx.enter_context(tc.tile_pool(name="keep", bufs=1))
         work = ctx.enter_context(tc.tile_pool(name="work", bufs=2))
-        stores = ctx.enter_context(tc.tile_pool(name="stores", bufs=6))
+        stores = ctx.enter_context(tc.tile_pool(name="stores", bufs=4))
         ps_plain = ctx.enter_context(tc.psum_pool(name="ps_plain", bufs=2))
         ps_acc = ctx.enter_context(tc.psum_pool(name="ps_acc", bufs=6))
 
@@ -92,20 +93,20 @@ def tile_edgefeaturenet_pa_t_kernel(
             out=w1_raw[64:96, :, :],
             in_=W1[2 * HID : 3 * HID, :].rearrange("(p t) c -> p t c", t=PACK),
         )
-        for g in range(2):
-            nc.sync.dma_start(
-                out=w1_raw[96:128, 2 * g : 2 * g + 2, :],
-                in_=W1[3 * HID + g * NB : 3 * HID + g * NB + 64, :].rearrange("(p e) c -> p e c", e=2),
-            )
+        nc.sync.dma_start(
+            out=w1_raw[96:128, :, :].rearrange("p (u e) c -> p u (e c)", u=2),
+            in_=W1[3 * HID : F, :].rearrange("(u p e) c -> p u (e c)", u=2, e=2),
+        )
         n2e_i = keep.tile([P, HID], BF16)
         nc.sync.dma_start(out=n2e_i[:], in_=n2e.rearrange("b i h -> (b i) h"))
         load_nodes(slice(0, JB))
-        nc.sync.dma_start(out=w1_raw[127:128, 1, :], in_=W1[F - 1 : F, :])
         b1_bf = keep.tile([P, E], BF16)
         nc.sync.dma_start(out=b1_bf[:], in_=b1.partition_broadcast(P))
         for first in range(JB, N, JL):
             load_emb(slice(first, first + JL))
             load_nodes(slice(first, first + JL))
+        b1_col = keep.tile([P, 1], BF16)
+        nc.sync.dma_start(out=b1_col[:], in_=b1[EP:E].unsqueeze(1))
 
         ident = keep.tile([P, P], BF16)
         make_identity(nc, ident[:])
@@ -126,12 +127,15 @@ def tile_edgefeaturenet_pa_t_kernel(
             bin_row[:], pattern=[[1, 64]], base=0, channel_multiplier=0,
             allow_small_or_imprecise_dtypes=True,
         )
+        corner_row = keep.tile([P, 2], BF16)
+        nc.gpsimd.memset(corner_row[:, 0:1], NB - 1.0)
+        nc.gpsimd.memset(corner_row[:, 1:2], 0.0)
         flags = keep.tile([P, N, 2], BF16)
         for b in range(B):
             rows = slice(b * N, (b + 1) * N)
-            nc.gpsimd.tensor_copy(out=flags[rows, :, 0:1], in_=flow_all[rows, b, :].unsqueeze(2))
+            nc.gpsimd.tensor_copy(out=flags[rows, :, 1:2], in_=flow_all[rows, b, :].unsqueeze(2))
         nc.gpsimd.tensor_copy(
-            out=flags[:, :, 1:2], in_=flow_i[:].unsqueeze(1).to_broadcast([P, N, 1])
+            out=flags[:, :, 0:1], in_=flow_i[:].unsqueeze(1).to_broadcast([P, N, 1])
         )
         zero = keep.tile([P, 1], F32)
         nc.vector.memset(zero[:], 0.0)
@@ -202,20 +206,27 @@ def tile_edgefeaturenet_pa_t_kernel(
                 op=ALU.add,
             )
 
-        def distograms(js):
+        def most_bins(js):
             count = js.stop - js.start
             for g in range(2):
                 nc.vector.tensor_tensor(
-                    out=halves[:, js, g, EDGE:HALF].rearrange("p j (w e) -> p j w e", e=2),
-                    in0=bin_pair[:, g, js, :].unsqueeze(2).to_broadcast([P, count, 32, 2]),
-                    in1=bin_row[:].rearrange("p (w e) -> p w e", e=2).unsqueeze(1).to_broadcast(
-                        [P, count, 32, 2]
+                    out=halves[:, js, g, EDGE : HALF - 2].rearrange("p j (w e) -> p j w e", e=2),
+                    in0=bin_pair[:, g, js, :].unsqueeze(2).to_broadcast([P, count, 31, 2]),
+                    in1=bin_row[:, g : g + NB - 1].rearrange("p (w e) -> p w e", e=2).unsqueeze(1).to_broadcast(
+                        [P, count, 31, 2]
                     ),
                     op=ALU.is_equal,
                 )
-            nc.vector.tensor_copy(
-                out=halves[:, js, :, HALF - 1 : HALF], in_=flags[:, js, :].unsqueeze(3)
+
+        def last_columns(js):
+            count = js.stop - js.start
+            nc.vector.tensor_tensor(
+                out=halves[:, js, 0, HALF - 2 : HALF],
+                in0=bin_pair[:, :, js, 0].rearrange("p g j -> p j g"),
+                in1=corner_row[:].unsqueeze(1).to_broadcast([P, count, 2]),
+                op=ALU.is_equal,
             )
+            nc.vector.tensor_copy(out=halves[:, js, 1, HALF - 2 : HALF], in_=flags[:, js, :])
 
         emb_t_of = {}
         grouped_of = {}
@@ -224,8 +235,9 @@ def tile_edgefeaturenet_pa_t_kernel(
         def transpose_emb(batch):
             emb_t_ps = ps_plain.tile([P, JB, P], BF16, name="plain_bank")
             for a in range(JB):
-                nc.tensor.transpose(
-                    out=emb_t_ps[:, a, :], in_=emb[:, batch * JB + a, :], identity=ident[:]
+                nc.tensor.matmul(
+                    out=emb_t_ps[:, a, :], lhsT=emb[:, batch * JB + a, :], rhs=ident[:],
+                    start=True, stop=True,
                 )
             emb_t = work.tile([P, JB, P], BF16)
             nc.scalar.copy(out=emb_t[:], in_=emb_t_ps[:])
@@ -294,50 +306,97 @@ def tile_edgefeaturenet_pa_t_kernel(
             )
 
         result_of = {}
+        turned_of = {}
+
+        def is_turned(batch):
+            return 0 < batch < BATCHES - 1
+
+        def multiply_turned(batch):
+            result_of[batch] = stores.tile([P, JB, E], F32, name="result")
+            if not is_turned(batch):
+                return
+            codes, scales = codes_of[batch]
+            acc = ps_acc.tile([P, BANK], F32, name="acc")
+            nc.tensor.matmul_mx(
+                out=acc[:],
+                lhsT=w1_codes[:, EP:E].bitcast(FP8X4),
+                lhsT_scale=w1_scales[:, EP:E],
+                rhs=codes[:].bitcast(FP8X4),
+                rhs_scale=scales[:],
+                start=True,
+                stop=True,
+            )
+            turned = work.tile([P, JB * P], F32)
+            nc.scalar.activation(out=turned[:], in_=acc[:], func=ACT.Relu, bias=b1_col[:])
+            turned_of[batch] = turned
+
+        def turn_back(batch):
+            if not is_turned(batch):
+                return
+            acc = ps_acc.tile([P, JB, P], F32, name="acc")
+            for a in range(JB):
+                nc.tensor.transpose(
+                    out=acc[:, a, :], in_=turned_of[batch][:, a * P : (a + 1) * P],
+                    identity=ident_words[:],
+                )
+            nc.scalar.copy(out=result_of[batch][:, :, EP:E], in_=acc[:])
 
         def multiply(batch, a0):
             codes, scales = codes_of[batch]
-            result = stores.tile([P, JS, E], F32)
-            for a in range(JS):
-                pairs = slice((a0 + a) * P, (a0 + a + 1) * P)
-                for e0 in range(0, E, BANK):
-                    acc = ps_acc.tile([P, BANK], F32)
-                    nc.tensor.matmul_mx(
-                        out=acc[:],
-                        lhsT=codes[:, pairs].bitcast(FP8X4),
-                        lhsT_scale=scales[:, pairs],
-                        rhs=w1_codes[:, e0 : e0 + BANK].bitcast(FP8X4),
-                        rhs_scale=w1_scales[:, e0 : e0 + BANK],
-                        start=True,
-                        stop=True,
-                    )
+            result = result_of[batch]
+            second = [BANK // 2, BANK // 4] if is_turned(batch) else [BANK]
+            for a in range(a0, a0 + JS):
+                pairs = slice(a * P, (a + 1) * P)
+                for first, widths in ((0, [BANK]), (BANK, second)):
+                    acc = ps_acc.tile([P, BANK], F32, name="acc")
+                    done = 0
+                    for width in widths:
+                        e0 = first + done
+                        nc.tensor.matmul_mx(
+                            out=acc[:, done : done + width],
+                            lhsT=codes[:, pairs].bitcast(FP8X4),
+                            lhsT_scale=scales[:, pairs],
+                            rhs=w1_codes[:, e0 : e0 + width].bitcast(FP8X4),
+                            rhs_scale=w1_scales[:, e0 : e0 + width],
+                            start=True,
+                            stop=True,
+                        )
+                        done += width
                     nc.vector.tensor_tensor(
-                        out=result[:, a, e0 : e0 + BANK], in0=acc[:],
-                        in1=b1_bf[:, e0 : e0 + BANK], op=ALU.add,
+                        out=result[:, a, first : first + done], in0=acc[:, 0:done],
+                        in1=b1_bf[:, first : first + done], op=ALU.add,
                     )
-            result_of[batch, a0] = result
 
-        def finish(batch, a0):
-            result = result_of[batch, a0]
-            last = batch == BATCHES - 1 and a0 == JB - JS
-            j0 = batch * JB + a0
-            if last:
-                relu_on_scalar(result[:, 0, :])
-                nc.sync.dma_start(out=out_rows[:, j0, :], in_=result[:, 0, :])
-                relu_on_scalar(result[:, 1, 0:BANK])
+        def relu(batch, a0):
+            result = result_of[batch]
+            end = EP if is_turned(batch) else E
+            if batch == BATCHES - 1 and a0 == JB - JS:
+                relu_on_scalar(result[:, a0, :])
+                relu_on_scalar(result[:, a0 + 1, 0:BANK])
                 nc.vector.tensor_scalar_max(
-                    out=result[:, 1, BANK:E], in0=result[:, 1, BANK:E], scalar1=0.0
+                    out=result[:, a0 + 1, BANK:E], in0=result[:, a0 + 1, BANK:E], scalar1=0.0
                 )
-                nc.sync.dma_start(out=out_rows[:, j0 + 1, :], in_=result[:, 1, :])
+                return
+            if is_turned(batch) and a0 > 0:
+                relu_on_gpsimd(result[:, a0, 0:end])
             else:
-                relu_on_scalar(result[:, 0, :])
-                relu_on_gpsimd(result[:, 1, :])
-                nc.sync.dma_start(out=out_rows[:, j0 : j0 + JS, :], in_=result[:])
+                relu_on_scalar(result[:, a0, 0:end])
+            relu_on_gpsimd(result[:, a0 + 1, 0:end])
+
+        def store(batch, a0):
+            j0 = batch * JB + a0
+            step = 1 if batch == BATCHES - 1 and a0 == JB - JS else JS
+            for a in range(0, JS, step):
+                nc.sync.dma_start(
+                    out=out_rows[:, j0 + a : j0 + a + step, :],
+                    in_=result_of[batch][:, a0 + a : a0 + a + step, :],
+                )
 
         transpose_emb(0)
         root_of_distances()
         bins_of_distances()
-        distograms(slice(0, JB))
+        most_bins(slice(0, JB))
+        last_columns(slice(0, JB))
         embedding_features(0)
         node_features(0)
         features_to_partitions(0)
@@ -356,34 +415,43 @@ def tile_edgefeaturenet_pa_t_kernel(
                 in_=w1_grouped[:, e0 : e0 + BANK, :].rearrange("p e t -> p (e t)"),
             )
         quantise(0)
-        distograms(slice(JB, 4 * JB))
+        last_columns(slice(JB, N))
+        most_bins(slice(JB, 4 * JB))
         transpose_emb(1)
         node_features(1)
         embedding_features(1)
         transpose_emb(2)
 
         for batch in range(BATCHES):
+            multiply_turned(batch)
             multiply(batch, 0)
             if batch == 0:
                 features_to_partitions(1)
                 node_features(2)
                 embedding_features(2)
                 transpose_emb(3)
-                finish(batch, 0)
-                distograms(slice(4 * JB, 10 * JB))
+                relu(batch, 0)
+                store(batch, 0)
+                most_bins(slice(4 * JB, 10 * JB))
                 quantise(1)
                 multiply(batch, JS)
-                distograms(slice(10 * JB, N))
+                most_bins(slice(10 * JB, N))
             if batch + 3 < BATCHES:
                 node_features(batch + 3)
                 embedding_features(batch + 3)
             if batch + 4 < BATCHES:
                 transpose_emb(batch + 4)
             if batch > 0:
-                finish(batch, 0)
+                relu(batch, 0)
+                if batch == BATCHES - 1:
+                    store(batch, 0)
                 if batch + 1 < BATCHES:
                     quantise(batch + 1)
                 multiply(batch, JS)
+            turn_back(batch)
+            if 0 < batch < BATCHES - 1:
+                store(batch, 0)
             if batch + 2 < BATCHES:
                 features_to_partitions(batch + 2)
-            finish(batch, JS)
+            relu(batch, JS)
+            store(batch, JS)

from contextlib import ExitStack

import concourse.mybir as mybir
from concourse.masks import make_identity

F32 = mybir.dt.float32
BF16 = mybir.dt.bfloat16
U32 = mybir.dt.uint32
I32 = mybir.dt.int32
U8 = mybir.dt.uint8
FP8X4 = mybir.dt.float8_e4m3fn_x4
ALU = mybir.AluOpType
ACT = mybir.ActivationFunctionType

B, N, XYZ, HID, NB, E = 2, 64, 3, 128, 63, 1024
F = 3 * HID + 2 * NB + 2
MIN_BIN, MAX_BIN, FAR = 0.001, 20.0, 1e8

P = 128
PACK = 4
BANK = 512
JB = 4
JS = 2
EP = E - P
JL = (N - JB) // 3
HALF = F // 2
EDGE = HID + 64
BATCHES = N // JB

FLOPS = 2 * B * N * N * F * E + 2 * B * N * N * HID * HID


BIN = (MAX_BIN - MIN_BIN) / (NB - 1)
BIN_HIGH = 41.0 / 128.0


def tile_edgefeaturenet_pa_t_kernel(
    tc, n2e, relpos_emb, trans, sc_trans, flow_mask, W_rp, b_rp, W1, b1, out
):
    nc = tc.nc
    emb_rows = relpos_emb.rearrange("b i j c -> (b i) j c")
    out_rows = out.rearrange("b i j e -> (b i) j e")

    with ExitStack() as ctx:
        ctx.enter_context(tc.manual_schedule())
        keep = ctx.enter_context(tc.tile_pool(name="keep", bufs=1))
        work = ctx.enter_context(tc.tile_pool(name="work", bufs=2))
        stores = ctx.enter_context(tc.tile_pool(name="stores", bufs=4))
        ps_plain = ctx.enter_context(tc.psum_pool(name="ps_plain", bufs=2))
        ps_acc = ctx.enter_context(tc.psum_pool(name="ps_acc", bufs=6))

        emb = keep.tile([P, N, HID], BF16)
        pm = keep.tile([P, N, F], BF16)
        halves = pm[:].rearrange("p j (u k) -> p j u k", u=2)

        def load_emb(js):
            nc.sync.dma_start(out=emb[:, js, :], in_=emb_rows[:, js, :])

        def load_nodes(js):
            for b in range(B):
                nc.sync.dma_start(
                    out=pm[b * N : (b + 1) * N, js, HALF : HALF + HID],
                    in_=n2e[b, js, :].partition_broadcast(N),
                )

        load_emb(slice(0, JB))
        pos_all = keep.tile([P, 2, B, N, XYZ], BF16)
        posi = keep.tile([P, 2, 16], BF16)
        for g, pos in enumerate((trans, sc_trans)):
            nc.scalar.dma_start(
                out=pos_all[:, g, :, :, :].rearrange("p b j c -> p (b j c)"),
                in_=pos.rearrange("b j c -> (b j c)").partition_broadcast(P),
            )
            nc.scalar.dma_start(out=posi[:, g, 0:XYZ], in_=pos.rearrange("b i c -> (b i) c"))
        flow_i = keep.tile([P, 1], BF16)
        nc.scalar.dma_start(out=flow_i[:], in_=flow_mask.rearrange("b i -> (b i)").unsqueeze(1))
        flow_all = keep.tile([P, B, N], BF16)
        nc.scalar.dma_start(
            out=flow_all[:].rearrange("p b j -> p (b j)"),
            in_=flow_mask.rearrange("b j -> (b j)").partition_broadcast(P),
        )
        wrp = keep.tile([P, HID], BF16)
        nc.sync.dma_start(out=wrp[:], in_=W_rp)
        brp_row = keep.tile([P, HID], BF16)
        nc.vector.memset(brp_row[:], 0.0)
        nc.sync.dma_start(out=brp_row[0:1, :], in_=b_rp.unsqueeze(0))
        w1_raw = keep.tile([P, PACK, E], BF16)
        nc.sync.dma_start(
            out=w1_raw[0:64, :, :].rearrange("p (u e) c -> p u (e c)", u=2),
            in_=W1[0 : 2 * HID, :].rearrange("(u p e) c -> p u (e c)", u=2, e=2),
        )
        nc.sync.dma_start(
            out=w1_raw[64:96, :, :],
            in_=W1[2 * HID : 3 * HID, :].rearrange("(p t) c -> p t c", t=PACK),
        )
        nc.sync.dma_start(
            out=w1_raw[96:128, :, :].rearrange("p (u e) c -> p u (e c)", u=2),
            in_=W1[3 * HID : F, :].rearrange("(u p e) c -> p u (e c)", u=2, e=2),
        )
        n2e_i = keep.tile([P, HID], BF16)
        nc.sync.dma_start(out=n2e_i[:], in_=n2e.rearrange("b i h -> (b i) h"))
        load_nodes(slice(0, JB))
        b1_bf = keep.tile([P, E], BF16)
        nc.sync.dma_start(out=b1_bf[:], in_=b1.partition_broadcast(P))
        for first in range(JB, N, JL):
            load_emb(slice(first, first + JL))
            load_nodes(slice(first, first + JL))
        b1_col = keep.tile([P, 1], BF16)
        nc.sync.dma_start(out=b1_col[:], in_=b1[EP:E].unsqueeze(1))

        ident = keep.tile([P, P], BF16)
        make_identity(nc, ident[:])
        ident_words = keep.tile([P, P], F32)
        make_identity(nc, ident_words[:])
        wrp_words = keep.tile([P, HID], BF16)
        brp_words = keep.tile([P, HID], BF16)
        for source, ordered in ((wrp, wrp_words), (brp_row, brp_words)):
            nc.gpsimd.tensor_copy(
                out=ordered[:].rearrange("p (u w e) -> p u w e", u=2, e=2),
                in_=source[:].rearrange("p (w u e) -> p u w e", u=2, e=2),
            )
        ones_row = keep.tile([P, P], BF16)
        nc.vector.memset(ones_row[:], 0.0)
        nc.vector.memset(ones_row[0:1, :], 1.0)
        bin_row = keep.tile([P, 64], BF16)
        nc.gpsimd.iota(
            bin_row[:], pattern=[[1, 64]], base=0, channel_multiplier=0,
            allow_small_or_imprecise_dtypes=True,
        )
        corner_row = keep.tile([P, 2], BF16)
        nc.gpsimd.memset(corner_row[:, 0:1], NB - 1.0)
        nc.gpsimd.memset(corner_row[:, 1:2], 0.0)
        flags = keep.tile([P, N, 2], BF16)
        for b in range(B):
            rows = slice(b * N, (b + 1) * N)
            nc.gpsimd.tensor_copy(out=flags[rows, :, 1:2], in_=flow_all[rows, b, :].unsqueeze(2))
        nc.gpsimd.tensor_copy(
            out=flags[:, :, 0:1], in_=flow_i[:].unsqueeze(1).to_broadcast([P, N, 1])
        )
        zero = keep.tile([P, 1], F32)
        nc.vector.memset(zero[:], 0.0)
        nc.scalar.activation(out=zero[:], in_=zero[:], func=ACT.Sqrt)

        diff = keep.tile([P, 2, N, XYZ], F32)
        for b in range(B):
            rows = slice(b * N, (b + 1) * N)
            nc.vector.tensor_tensor(
                out=diff[rows, :, :, :],
                in0=pos_all[rows, :, b, :, :],
                in1=posi[rows, :, 0:XYZ].unsqueeze(2).to_broadcast([N, 2, N, XYZ]),
                op=ALU.subtract,
            )
        nc.vector.tensor_tensor(out=diff[:], in0=diff[:], in1=diff[:], op=ALU.mult)
        dist_sq = keep.tile([P, 2, N], F32)
        nc.vector.tensor_reduce(out=dist_sq[:], in_=diff[:], axis=mybir.AxisListType.X, op=ALU.add)
        root = keep.tile([P, 2, N], F32)
        near = keep.tile([P, 2, N], I32)
        edge = keep.tile([P, 2, N], F32)
        edge_low = keep.tile([P, 2, N], F32)
        edge_sq = keep.tile([P, 2, N], F32)
        rest = keep.tile([P, 2, N], F32)
        beyond = keep.tile([P, 2, N], F32)
        on_edge = keep.tile([P, 2, N], F32)
        bin_of = keep.tile([P, 2, N], F32)
        bin_pair = keep.tile([P, 2, N, 2], BF16)

        def root_of_distances():
            nc.scalar.activation(
                out=root[:], in_=dist_sq[:], func=ACT.Sqrt, scale=1.0 / (BIN * BIN)
            )

        def bins_of_distances():
            nc.vector.tensor_scalar(
                out=near[:], in0=root[:], scalar1=0.25 - MIN_BIN / BIN, scalar2=NB - 1 + 0.3,
                op0=ALU.add, op1=ALU.min,
            )
            nc.vector.tensor_scalar(
                out=on_edge[:], in0=dist_sq[:], scalar1=MAX_BIN * MAX_BIN, scalar2=0.5,
                op0=ALU.is_equal, op1=ALU.mult,
            )
            nc.vector.tensor_scalar(
                out=edge[:], in0=near[:], scalar1=BIN_HIGH, scalar2=0.0, op0=ALU.mult, op1=ALU.add
            )
            nc.vector.tensor_scalar(
                out=edge_low[:], in0=near[:], scalar1=BIN - BIN_HIGH, scalar2=MIN_BIN,
                op0=ALU.mult, op1=ALU.add,
            )
            nc.vector.scalar_tensor_tensor(
                out=on_edge[:], in0=dist_sq[:], scalar=FAR * FAR, in1=on_edge[:],
                op0=ALU.is_ge, op1=ALU.add,
            )
            nc.vector.tensor_tensor(out=edge_sq[:], in0=edge[:], in1=edge[:], op=ALU.mult)
            nc.vector.scalar_tensor_tensor(
                out=rest[:], in0=edge[:], scalar=2.0, in1=edge_low[:], op0=ALU.mult, op1=ALU.add
            )
            nc.vector.tensor_tensor(out=edge_sq[:], in0=dist_sq[:], in1=edge_sq[:], op=ALU.subtract)
            nc.vector.tensor_tensor(out=rest[:], in0=rest[:], in1=edge_low[:], op=ALU.mult)
            nc.vector.scalar_tensor_tensor(
                out=on_edge[:], in0=near[:], scalar=-1.0, in1=on_edge[:], op0=ALU.add, op1=ALU.add
            )
            nc.vector.tensor_tensor(out=beyond[:], in0=edge_sq[:], in1=rest[:], op=ALU.is_gt)
            nc.vector.tensor_tensor(
                out=bin_pair[:],
                in0=beyond[:].unsqueeze(3).to_broadcast([P, 2, N, 2]),
                in1=on_edge[:].unsqueeze(3).to_broadcast([P, 2, N, 2]),
                op=ALU.add,
            )

        def most_bins(js):
            count = js.stop - js.start
            for g in range(2):
                nc.vector.tensor_tensor(
                    out=halves[:, js, g, EDGE : HALF - 2].rearrange("p j (w e) -> p j w e", e=2),
                    in0=bin_pair[:, g, js, :].unsqueeze(2).to_broadcast([P, count, 31, 2]),
                    in1=bin_row[:, g : g + NB - 1].rearrange("p (w e) -> p w e", e=2).unsqueeze(1).to_broadcast(
                        [P, count, 31, 2]
                    ),
                    op=ALU.is_equal,
                )

        def last_columns(js):
            count = js.stop - js.start
            nc.vector.tensor_tensor(
                out=halves[:, js, 0, HALF - 2 : HALF],
                in0=bin_pair[:, :, js, 0].rearrange("p g j -> p j g"),
                in1=corner_row[:].unsqueeze(1).to_broadcast([P, count, 2]),
                op=ALU.is_equal,
            )
            nc.vector.tensor_copy(out=halves[:, js, 1, HALF - 2 : HALF], in_=flags[:, js, :])

        emb_t_of = {}
        grouped_of = {}
        codes_of = {}

        def transpose_emb(batch):
            emb_t_ps = ps_plain.tile([P, JB, P], BF16, name="plain_bank")
            for a in range(JB):
                nc.tensor.matmul(
                    out=emb_t_ps[:, a, :], lhsT=emb[:, batch * JB + a, :], rhs=ident[:],
                    start=True, stop=True,
                )
            emb_t = work.tile([P, JB, P], BF16)
            nc.scalar.copy(out=emb_t[:], in_=emb_t_ps[:])
            emb_t_of[batch] = emb_t

        def node_features(batch):
            js = slice(batch * JB, (batch + 1) * JB)
            nc.scalar.copy(
                out=pm[:, js, 0:HID], in_=n2e_i[:].unsqueeze(1).to_broadcast([P, JB, HID])
            )

        def embedding_features(batch):
            js = slice(batch * JB, (batch + 1) * JB)
            emb_t = emb_t_of[batch]
            rel_ps = ps_plain.tile([P, JB, HID], F32, name="plain_bank")
            for a in range(JB):
                nc.tensor.matmul(
                    out=rel_ps[:, a, :], lhsT=ones_row[:], rhs=brp_words[:], start=True, stop=False
                )
                nc.tensor.matmul(
                    out=rel_ps[:, a, :], lhsT=emb_t[:, a, :], rhs=wrp_words[:], start=False, stop=True
                )
            nc.scalar.copy(
                out=halves[:, js, :, HID:EDGE],
                in_=rel_ps[:].rearrange("p a (u k) -> p a u k", u=2),
            )

        def features_to_partitions(batch):
            pm_words = pm[:, batch * JB : (batch + 1) * JB, :].rearrange("p a k -> p (a k)").bitcast(F32)
            grouped = work.tile([P, JB, P, PACK], BF16, align_bytes=64)
            grouped_words = grouped[:].rearrange("p a n t -> p (a n t)").bitcast(F32)
            for a0 in range(0, JB, 2):
                feat_ps = ps_plain.tile([P, 2, 2, P], F32, name="plain_bank")
                for a in range(2):
                    for u in range(2):
                        w0 = ((a0 + a) * 2 + u) * P
                        nc.tensor.transpose(
                            out=feat_ps[:, a, u, :], in_=pm_words[:, w0 : w0 + P],
                            identity=ident_words[:],
                        )
                nc.scalar.copy(
                    out=grouped_words[:, a0 * 2 * P : (a0 + 2) * 2 * P].rearrange(
                        "p (a n u) -> p a n u", a=2, u=2
                    ),
                    in_=feat_ps[:].rearrange("p a u n -> p a n u"),
                )
            grouped_of[batch] = grouped

        def quantise(batch):
            grouped = grouped_of[batch]
            codes = work.tile([P, JB * P], U32, align_bytes=64)
            scales = work.tile([P, JB * P], U8, align_bytes=64)
            nc.vector.quantize_mx(
                out=codes[:].bitcast(FP8X4),
                scales=scales[:],
                in_=grouped[:].rearrange("p a n t -> p (a n t)"),
            )
            codes_of[batch] = (codes, scales)

        def relu_on_scalar(values):
            nc.scalar.activation(out=values, in_=values, func=ACT.Relu)

        def relu_on_gpsimd(values):
            nc.gpsimd.tensor_scalar(
                out=values, in0=values, scalar1=float("inf"), scalar2=0.0, op0=ALU.min, op1=ALU.max
            )

        result_of = {}
        turned_of = {}

        def is_turned(batch):
            return 0 < batch < BATCHES - 1

        def multiply_turned(batch):
            result_of[batch] = stores.tile([P, JB, E], F32, name="result")
            if not is_turned(batch):
                return
            codes, scales = codes_of[batch]
            acc = ps_acc.tile([P, BANK], F32, name="acc")
            nc.tensor.matmul_mx(
                out=acc[:],
                lhsT=w1_codes[:, EP:E].bitcast(FP8X4),
                lhsT_scale=w1_scales[:, EP:E],
                rhs=codes[:].bitcast(FP8X4),
                rhs_scale=scales[:],
                start=True,
                stop=True,
            )
            turned = work.tile([P, JB * P], F32)
            nc.scalar.activation(out=turned[:], in_=acc[:], func=ACT.Relu, bias=b1_col[:])
            turned_of[batch] = turned

        def turn_back(batch):
            if not is_turned(batch):
                return
            acc = ps_acc.tile([P, JB, P], F32, name="acc")
            for a in range(JB):
                nc.tensor.transpose(
                    out=acc[:, a, :], in_=turned_of[batch][:, a * P : (a + 1) * P],
                    identity=ident_words[:],
                )
            nc.scalar.copy(out=result_of[batch][:, :, EP:E], in_=acc[:])

        def multiply(batch, a0):
            codes, scales = codes_of[batch]
            result = result_of[batch]
            second = [BANK // 2, BANK // 4] if is_turned(batch) else [BANK]
            for a in range(a0, a0 + JS):
                pairs = slice(a * P, (a + 1) * P)
                for first, widths in ((0, [BANK]), (BANK, second)):
                    acc = ps_acc.tile([P, BANK], F32, name="acc")
                    done = 0
                    for width in widths:
                        e0 = first + done
                        nc.tensor.matmul_mx(
                            out=acc[:, done : done + width],
                            lhsT=codes[:, pairs].bitcast(FP8X4),
                            lhsT_scale=scales[:, pairs],
                            rhs=w1_codes[:, e0 : e0 + width].bitcast(FP8X4),
                            rhs_scale=w1_scales[:, e0 : e0 + width],
                            start=True,
                            stop=True,
                        )
                        done += width
                    nc.vector.tensor_tensor(
                        out=result[:, a, first : first + done], in0=acc[:, 0:done],
                        in1=b1_bf[:, first : first + done], op=ALU.add,
                    )

        def relu(batch, a0):
            result = result_of[batch]
            end = EP if is_turned(batch) else E
            if batch == BATCHES - 1 and a0 == JB - JS:
                relu_on_scalar(result[:, a0, :])
                relu_on_scalar(result[:, a0 + 1, 0:BANK])
                nc.vector.tensor_scalar_max(
                    out=result[:, a0 + 1, BANK:E], in0=result[:, a0 + 1, BANK:E], scalar1=0.0
                )
                return
            if is_turned(batch) and a0 > 0:
                relu_on_gpsimd(result[:, a0, 0:end])
            else:
                relu_on_scalar(result[:, a0, 0:end])
            relu_on_gpsimd(result[:, a0 + 1, 0:end])

        def store(batch, a0):
            j0 = batch * JB + a0
            step = 1 if batch == BATCHES - 1 and a0 == JB - JS else JS
            for a in range(0, JS, step):
                nc.sync.dma_start(
                    out=out_rows[:, j0 + a : j0 + a + step, :],
                    in_=result_of[batch][:, a0 + a : a0 + a + step, :],
                )

        transpose_emb(0)
        root_of_distances()
        bins_of_distances()
        most_bins(slice(0, JB))
        last_columns(slice(0, JB))
        embedding_features(0)
        node_features(0)
        features_to_partitions(0)
        w1_grouped = keep.tile([P, E, PACK], BF16, align_bytes=64)
        w1_codes = keep.tile([P, E], U32, align_bytes=64)
        w1_scales = keep.tile([P, E], U8, align_bytes=64)
        for e0 in range(0, E, BANK):
            nc.vector.tensor_copy(
                out=w1_grouped[:, e0 : e0 + BANK, :].rearrange("p (c i) t -> p c t i", i=PACK),
                in_=w1_raw[:, :, e0 : e0 + BANK].rearrange("p t (c i) -> p c t i", i=PACK),
            )
        for e0 in range(0, E, BANK):
            nc.vector.quantize_mx(
                out=w1_codes[:, e0 : e0 + BANK].bitcast(FP8X4),
                scales=w1_scales[:, e0 : e0 + BANK],
                in_=w1_grouped[:, e0 : e0 + BANK, :].rearrange("p e t -> p (e t)"),
            )
        quantise(0)
        last_columns(slice(JB, N))
        most_bins(slice(JB, 4 * JB))
        transpose_emb(1)
        node_features(1)
        embedding_features(1)
        transpose_emb(2)

        for batch in range(BATCHES):
            multiply_turned(batch)
            multiply(batch, 0)
            if batch == 0:
                features_to_partitions(1)
                node_features(2)
                embedding_features(2)
                transpose_emb(3)
                relu(batch, 0)
                store(batch, 0)
                most_bins(slice(4 * JB, 10 * JB))
                quantise(1)
                multiply(batch, JS)
                most_bins(slice(10 * JB, N))
            if batch + 3 < BATCHES:
                node_features(batch + 3)
                embedding_features(batch + 3)
            if batch + 4 < BATCHES:
                transpose_emb(batch + 4)
            if batch > 0:
                relu(batch, 0)
                if batch == BATCHES - 1:
                    store(batch, 0)
                if batch + 1 < BATCHES:
                    quantise(batch + 1)
                multiply(batch, JS)
            turn_back(batch)
            if 0 < batch < BATCHES - 1:
                store(batch, 0)
            if batch + 2 < BATCHES:
                features_to_partitions(batch + 2)
            relu(batch, JS)
            store(batch, JS)
